import numpy as np
import ml_dtypes


def mxq(x, axis, fmt="e4m3"):
    dtype, down = {"e4m3": (ml_dtypes.float8_e4m3fn, 7), "e5m2": (ml_dtypes.float8_e5m2, 14)}[fmt]
    v = np.moveaxis(np.asarray(x, np.float32).astype(ml_dtypes.bfloat16).astype(np.float64), axis, -1)
    blocks = v.reshape(v.shape[:-1] + (-1, 32))
    amax = np.abs(blocks).max(-1, keepdims=True)
    byte = np.maximum(np.where(amax > 0, np.frexp(amax)[1] - 1 + 127, 0) - down, 1)
    scale = np.exp2(byte - 127.0)
    codes = (blocks / scale).astype(np.float32).astype(dtype).astype(np.float64)
    return np.moveaxis((codes * scale).reshape(v.shape), -1, axis)


WIDE = False


def mx_kscale(k):
    if not WIDE:
        return np.ones(k)
    levels = np.array([10, -10, 5, -5, 0])
    a = np.random.permutation(np.resize(levels, k // 512 * 4)).reshape(k // 512, 4)
    idx = np.arange(k)
    return np.exp2(a[idx // 512, idx % 128 // 32])


BF16 = ml_dtypes.bfloat16


def bf(x):
    return np.asarray(x, np.float32).astype(BF16)


def f64(x):
    return np.asarray(x).astype(np.float64)


B, SQ, SK, D, DK, L = 2, 2048, 512, 512, 64, 10000
SCALE = np.sqrt(2.0 * DK)


def setup_inputs():
    s = mx_kscale(D)
    a = np.sqrt(1.4 * SCALE / np.sqrt(D))
    return {"q": bf(np.random.standard_normal((B, SQ, D)) * a * s),
            "k": bf(np.random.standard_normal((B, SK, D)) * a / s),
            "v": bf(np.random.standard_normal((B, SK, D)) * 2.0),
            "pos_bias": bf(np.random.standard_normal((SQ, SK)) * SCALE)}


def reference(q, k, v, pos_bias):
    scores = mxq(f64(q), 2, "e4m3") @ mxq(f64(k), 2, "e4m3").transpose(0, 2, 1)
    scores = scores + f64(pos_bias)[None, :, :]
    scores = scores / SCALE
    e = np.exp(scores - scores.max(-1, keepdims=True))
    attn = e / e.sum(-1, keepdims=True)
    context = mxq(attn, 2, "e4m3") @ mxq(f64(v), 1, "e4m3")
    context = np.swapaxes(context, 1, 2).reshape(B, -1, D)
    return context, attn

@@ -1,0 +1,243 @@
+import math
+from contextlib import ExitStack
+
+import concourse.masks as masks
+import concourse.mybir as mybir
+
+F32 = mybir.dt.float32
+BF16 = mybir.dt.bfloat16
+U32 = mybir.dt.uint32
+U8 = mybir.dt.uint8
+FP8X4 = mybir.dt.float8_e4m3fn_x4
+ALU = mybir.AluOpType
+EXP = mybir.ActivationFunctionType.Exp
+AXIS_X = mybir.AxisListType.X
+
+B, SQ, SK, D = 2, 2048, 512, 512
+P = 128
+PACK = 4
+GROUP = 4
+TILES_PER_BATCH = SQ // P
+N_TILES = B * TILES_PER_BATCH
+INV_SCALE = 1.0 / math.sqrt(2.0 * 64.0)
+
+FLOPS = 2 * (2 * B * SQ * SK * D)
+
+
+def tile_multiheadattention_tupe_pb_t_kernel(tc, q, k, v, pos_bias, out_0, out_1):
+    nc = tc.nc
+    with ExitStack() as ctx:
+        ctx.enter_context(tc.manual_schedule())
+        const = ctx.enter_context(tc.tile_pool(name="const", bufs=1))
+        inputs = ctx.enter_context(tc.tile_pool(name="inputs", bufs=1))
+        keep = ctx.enter_context(tc.tile_pool(name="keep", bufs=1))
+        work = ctx.enter_context(tc.tile_pool(name="work", bufs=4))
+        results = ctx.enter_context(tc.tile_pool(name="results", bufs=3))
+        psum = ctx.enter_context(tc.psum_pool(name="psum", bufs=2))
+
+        def place(n):
+            return n // TILES_PER_BATCH, (n % TILES_PER_BATCH) // GROUP, n % GROUP
+
+        def group_rows(g):
+            return slice(g * GROUP * P, (g + 1) * GROUP * P)
+
+        q_sb, pos_sb, k_sb, v_sb = {}, {}, {}, {}
+
+        def load_rows(table, key, rows, name):
+            table[key] = inputs.tile([P, GROUP * 512], BF16, name=name)
+            nc.sync.dma_start(
+                out=table[key][:].rearrange("p (j d) -> p j d", j=GROUP),
+                in_=rows.rearrange("(j p) d -> p j d", p=P),
+            )
+
+        def load_q(b, g):
+            load_rows(q_sb, (b, g), q[b, group_rows(g), :], "q_sb_%d_%d" % (b, g))
+
+        def load_pos(g):
+            load_rows(pos_sb, g, pos_bias[group_rows(g), :], "pos_sb_%d" % g)
+
+        load_rows(k_sb, 0, k[0], "k_sb_0")
+        load_q(0, 0)
+        load_pos(0)
+        load_rows(v_sb, 0, v[0], "v_sb_0")
+        for g in range(1, TILES_PER_BATCH // GROUP):
+            load_q(0, g)
+            load_pos(g)
+        load_rows(k_sb, 1, k[1], "k_sb_1")
+        load_q(1, 0)
+        load_rows(v_sb, 1, v[1], "v_sb_1")
+        for g in range(1, TILES_PER_BATCH // GROUP):
+            load_q(1, g)
+
+        ident = const.tile([P, P], F32, name="ident")
+        masks.make_identity(nc, ident[:])
+        zero = const.tile([P, 1], F32, name="zero")
+        one = const.tile([P, 1], F32, name="one")
+        nc.vector.memset(zero[:], 0.0)
+        nc.scalar.activation(out=one[:], in_=zero[:], func=EXP)
+
+        def transpose_words(rows_sb, j):
+            words = rows_sb[:].bitcast(F32)
+            words_t = psum.tile([P, 2, P], F32, name="words_t")
+            for u in range(2):
+                first = (2 * j + u) * P
+                nc.tensor.transpose(words_t[:, u, :], words[:, first : first + P], ident[:])
+            return words_t
+
+        def regroup_words(copy, words_t, grouped):
+            copy(
+                out=grouped.bitcast(F32).rearrange("p (m u) -> p m u", u=2),
+                in_=words_t[:].rearrange("p u m -> p m u"),
+            )
+
+        def quantise(pool, name, width, grouped):
+            codes = pool.tile([P, width], U32, name=name + "_codes", align_bytes=64)
+            scales = pool.tile([P, width], U8, name=name + "_scales", align_bytes=64)
+            nc.vector.quantize_mx(out=codes[:].bitcast(FP8X4), scales=scales[:], in_=grouped)
+            return codes, scales
+
+        k_mx, v_mx = {}, {}
+
+        def prepare_k(b):
+            grouped = keep.tile([P, SK * PACK], BF16, name="k_grouped_%d" % b, align_bytes=64)
+            for t in range(SK // P):
+                words_t = transpose_words(k_sb[b], t)
+                copy = nc.vector.tensor_copy if t % 2 == 0 else nc.scalar.copy
+                regroup_words(copy, words_t, grouped[:, t * P * PACK : (t + 1) * P * PACK])
+            k_mx[b] = quantise(keep, "k%d" % b, SK, grouped[:])
+
+        def prepare_v(b):
+            grouped = keep.tile([P, D, PACK], BF16, name="v_grouped_%d" % b, align_bytes=64)
+            nc.vector.tensor_copy(out=grouped[:], in_=v_sb[b][:].rearrange("p (t d) -> p d t", t=PACK))
+            v_mx[b] = quantise(keep, "v%d" % b, D, grouped[:].rearrange("p d t -> p (d t)"))
+
+        t = {}
+
+        def q_transposes(n):
+            b, g, j = place(n)
+            if n % TILES_PER_BATCH == 0:
+                prepare_k(b)
+            t["words_t", n] = transpose_words(q_sb[(b, g)], j)
+
+        def q_regroup(n):
+            t["q_grouped", n] = work.tile([P, P * PACK], BF16, name="q_grouped", align_bytes=64)
+            regroup_words(nc.vector.tensor_copy, t["words_t", n], t["q_grouped", n][:])
+
+        def q_quantise(n):
+            t["q_mx", n] = quantise(work, "q", P, t["q_grouped", n][:])
+
+        def scores(n):
+            b, g, j = place(n)
+            q_codes, q_scales = t["q_mx", n]
+            k_codes, k_scales = k_mx[b]
+            t["score_ps", n] = psum.tile([P, SK], F32, name="score_ps")
+            nc.tensor.matmul_mx(
+                out=t["score_ps", n][:],
+                lhsT=q_codes[:].bitcast(FP8X4),
+                lhsT_scale=q_scales[:],
+                rhs=k_codes[:].bitcast(FP8X4),
+                rhs_scale=k_scales[:],
+                start=True,
+                stop=True,
+            )
+
+        def add_and_max(n):
+            b, g, j = place(n)
+            if n % TILES_PER_BATCH == 0:
+                prepare_v(b)
+            t["s_sb", n] = work.tile([P, SK], F32, name="s_sb")
+            row_max = work.tile([P, 1], F32, name="row_max")
+            t["exp_bias", n] = work.tile([P, 1], F32, name="exp_bias")
+            nc.vector.tensor_tensor(
+                out=t["s_sb", n][:], in0=t["score_ps", n][:],
+                in1=pos_sb[g][:, j * SK : (j + 1) * SK], op=ALU.add,
+            )
+            nc.vector.tensor_reduce(out=row_max[:], in_=t["s_sb", n][:], axis=AXIS_X, op=ALU.max)
+            nc.gpsimd.tensor_scalar(
+                out=t["exp_bias", n][:], in0=row_max[:],
+                scalar1=-INV_SCALE, scalar2=0.0, op0=ALU.mult, op1=ALU.add,
+            )
+
+        def exponent(n):
+            t["e_sb", n] = work.tile([P, SK], F32, name="e_sb")
+            t["row_sum", n] = work.tile([P, 1], F32, name="row_sum")
+            nc.scalar.activation(
+                out=t["e_sb", n][:], in_=t["s_sb", n][:], func=EXP,
+                bias=t["exp_bias", n][:], scale=INV_SCALE, accum_out=t["row_sum", n][:],
+            )
+
+        def normalise(n):
+            b, g, j = place(n)
+            if j == 0:
+                t["attn_sb", b, g] = results.tile([P, GROUP, SK], F32, name="attn_sb")
+            attn_sb = t["attn_sb", b, g]
+            inv_sum = work.tile([P, 1], F32, name="inv_sum")
+            nc.vector.reciprocal(out=inv_sum[:], in_=t["row_sum", n][:])
+            nc.gpsimd.tensor_scalar(
+                out=attn_sb[:, j, :], in0=t["e_sb", n][:],
+                scalar1=inv_sum[:], scalar2=0.0, op0=ALU.mult, op1=ALU.add,
+            )
+            if j == GROUP - 1:
+                nc.sync.dma_start(
+                    out=out_1[b, group_rows(g), :].rearrange("(j p) n -> p j n", p=P), in_=attn_sb[:]
+                )
+
+        def attn_transposes(n):
+            b, g, j = place(n)
+            t["attn_t", n] = psum.tile([P, PACK, P], F32, name="attn_t")
+            for x in range(PACK):
+                nc.tensor.transpose(
+                    t["attn_t", n][:, x, :], t["attn_sb", b, g][:, j, x * P : (x + 1) * P], ident[:]
+                )
+
+        def attn_regroup(n):
+            t["a_grouped", n] = work.tile([P, P, PACK], BF16, name="a_grouped", align_bytes=64)
+            nc.scalar.copy(out=t["a_grouped", n][:], in_=t["attn_t", n][:].rearrange("p x m -> p m x"))
+
+        def attn_quantise(n):
+            t["a_mx", n] = quantise(work, "a", P, t["a_grouped", n][:].rearrange("p m x -> p (m x)"))
+
+        def context_matmuls(n):
+            b, g, j = place(n)
+            a_codes, a_scales = t["a_mx", n]
+            v_codes, v_scales = v_mx[b]
+            t["ctx_ps", n] = psum.tile([P, D // P, P], F32, name="ctx_ps")
+            for f in range(D // P):
+                cols = slice(f * P, (f + 1) * P)
+                nc.tensor.matmul_mx(
+                    out=t["ctx_ps", n][:, f, :],
+                    lhsT=v_codes[:, cols].bitcast(FP8X4),
+                    lhsT_scale=v_scales[:, cols],
+                    rhs=a_codes[:].bitcast(FP8X4),
+                    rhs_scale=a_scales[:],
+                    start=True,
+                    stop=True,
+                )
+
+        def context_out(n):
+            b, g, j = place(n)
+            if j == 0:
+                t["ctx_sb", b, g] = results.tile([P, D // P, GROUP * P], F32, name="ctx_sb")
+            ctx_sb = t["ctx_sb", b, g]
+            nc.scalar.copy(out=ctx_sb[:, :, j * P : (j + 1) * P], in_=t["ctx_ps", n][:])
+            if j == GROUP - 1:
+                rows = out_0[b].rearrange("(f p g) n -> g p f n", p=P, g=TILES_PER_BATCH // GROUP)
+                nc.sync.dma_start(out=rows[g], in_=ctx_sb[:])
+
+        def run(stage, n):
+            if 0 <= n < N_TILES:
+                stage(n)
+
+        for step in range(-4, N_TILES + 6):
+            run(context_matmuls, step - 5)
+            run(scores, step + 1)
+            run(attn_transposes, step - 3)
+            run(q_transposes, step + 4)
+            run(normalise, step - 2)
+            run(add_and_max, step)
+            run(exponent, step - 1)
+            run(context_out, step - 5)
+            run(attn_regroup, step - 3)
+            run(attn_quantise, step - 4)
+            run(q_regroup, step + 3)
+            run(q_quantise, step + 2)

@@ -17,8 +17,10 @@ B, SQ, SK, D = 2, 2048, 512, 512
 P = 128
 PACK = 4
 GROUP = 4
+HALF = 2 * P * PACK
 TILES_PER_BATCH = SQ // P
 N_TILES = B * TILES_PER_BATCH
+CONTEXT_LAG = 12
 INV_SCALE = 1.0 / math.sqrt(2.0 * 64.0)
 
 FLOPS = 2 * (2 * B * SQ * SK * D)
@@ -27,7 +29,6 @@ FLOPS = 2 * (2 * B * SQ * SK * D)
 def tile_multiheadattention_tupe_pb_t_kernel(tc, q, k, v, pos_bias, out_0, out_1):
     nc = tc.nc
     with ExitStack() as ctx:
-        ctx.enter_context(tc.manual_schedule())
         const = ctx.enter_context(tc.tile_pool(name="const", bufs=1))
         inputs = ctx.enter_context(tc.tile_pool(name="inputs", bufs=1))
         keep = ctx.enter_context(tc.tile_pool(name="keep", bufs=1))
@@ -58,11 +59,13 @@ def tile_multiheadattention_tupe_pb_t_kernel(tc, q, k, v, pos_bias, out_0, out_1
 
         load_rows(k_sb, 0, k[0], "k_sb_0")
         load_q(0, 0)
+        load_q(0, 1)
         load_pos(0)
         load_rows(v_sb, 0, v[0], "v_sb_0")
-        for g in range(1, TILES_PER_BATCH // GROUP):
+        for g in range(2, TILES_PER_BATCH // GROUP):
             load_q(0, g)
-            load_pos(g)
+            load_pos(g - 1)
+        load_pos(TILES_PER_BATCH // GROUP - 1)
         load_rows(k_sb, 1, k[1], "k_sb_1")
         load_q(1, 0)
         load_rows(v_sb, 1, v[1], "v_sb_1")
@@ -76,18 +79,16 @@ def tile_multiheadattention_tupe_pb_t_kernel(tc, q, k, v, pos_bias, out_0, out_1
         nc.vector.memset(zero[:], 0.0)
         nc.scalar.activation(out=one[:], in_=zero[:], func=EXP)
 
-        def transpose_words(rows_sb, j):
+        def transpose_words(rows_sb, j, words_t):
             words = rows_sb[:].bitcast(F32)
-            words_t = psum.tile([P, 2, P], F32, name="words_t")
             for u in range(2):
                 first = (2 * j + u) * P
-                nc.tensor.transpose(words_t[:, u, :], words[:, first : first + P], ident[:])
-            return words_t
+                nc.tensor.transpose(words_t[:, j % 2, u, :], words[:, first : first + P], ident[:])
 
         def regroup_words(copy, words_t, grouped):
             copy(
-                out=grouped.bitcast(F32).rearrange("p (m u) -> p m u", u=2),
-                in_=words_t[:].rearrange("p u m -> p m u"),
+                out=grouped.bitcast(F32).rearrange("p (r m u) -> p r m u", r=2, u=2),
+                in_=words_t[:].rearrange("p r u m -> p r m u"),
             )
 
         def quantise(pool, name, width, grouped):
@@ -100,10 +101,12 @@ def tile_multiheadattention_tupe_pb_t_kernel(tc, q, k, v, pos_bias, out_0, out_1
 
         def prepare_k(b):
             grouped = keep.tile([P, SK * PACK], BF16, name="k_grouped_%d" % b, align_bytes=64)
-            for t in range(SK // P):
-                words_t = transpose_words(k_sb[b], t)
-                copy = nc.vector.tensor_copy if t % 2 == 0 else nc.scalar.copy
-                regroup_words(copy, words_t, grouped[:, t * P * PACK : (t + 1) * P * PACK])
+            for h in range(2):
+                words_t = psum.tile([P, 2, 2, P], F32, name="words_t")
+                transpose_words(k_sb[b], 2 * h, words_t)
+                transpose_words(k_sb[b], 2 * h + 1, words_t)
+                copy = nc.vector.tensor_copy if h == 0 else nc.scalar.copy
+                regroup_words(copy, words_t, grouped[:, h * HALF : (h + 1) * HALF])
             k_mx[b] = quantise(keep, "k%d" % b, SK, grouped[:])
 
         def prepare_v(b):
@@ -117,24 +120,36 @@ def tile_multiheadattention_tupe_pb_t_kernel(tc, q, k, v, pos_bias, out_0, out_1
             b, g, j = place(n)
             if n % TILES_PER_BATCH == 0:
                 prepare_k(b)
-            t["words_t", n] = transpose_words(q_sb[(b, g)], j)
+            if j % 2 == 0:
+                t["words_t", b, g, j // 2] = psum.tile([P, 2, 2, P], F32, name="words_t")
+            transpose_words(q_sb[(b, g)], j, t["words_t", b, g, j // 2])
 
         def q_regroup(n):
-            t["q_grouped", n] = work.tile([P, P * PACK], BF16, name="q_grouped", align_bytes=64)
-            regroup_words(nc.vector.tensor_copy, t["words_t", n], t["q_grouped", n][:])
+            b, g, j = place(n)
+            if j == 0:
+                t["q_grouped", b, g] = work.tile([P, GROUP * P * PACK], BF16, name="q_grouped", align_bytes=64)
+            if j % 2 == 1:
+                h = j // 2
+                regroup_words(
+                    nc.scalar.copy, t["words_t", b, g, h],
+                    t["q_grouped", b, g][:, h * HALF : (h + 1) * HALF],
+                )
 
         def q_quantise(n):
-            t["q_mx", n] = quantise(work, "q", P, t["q_grouped", n][:])
+            b, g, j = place(n)
+            if j == GROUP - 1:
+                t["q_mx", b, g] = quantise(work, "q", GROUP * P, t["q_grouped", b, g][:])
 
         def scores(n):
             b, g, j = place(n)
-            q_codes, q_scales = t["q_mx", n]
+            q_codes, q_scales = t["q_mx", b, g]
             k_codes, k_scales = k_mx[b]
+            cols = slice(j * P, (j + 1) * P)
             t["score_ps", n] = psum.tile([P, SK], F32, name="score_ps")
             nc.tensor.matmul_mx(
                 out=t["score_ps", n][:],
-                lhsT=q_codes[:].bitcast(FP8X4),
-                lhsT_scale=q_scales[:],
+                lhsT=q_codes[:, cols].bitcast(FP8X4),
+                lhsT_scale=q_scales[:, cols],
                 rhs=k_codes[:].bitcast(FP8X4),
                 rhs_scale=k_scales[:],
                 start=True,
@@ -191,53 +206,60 @@ def tile_multiheadattention_tupe_pb_t_kernel(tc, q, k, v, pos_bias, out_0, out_1
                 )
 
         def attn_regroup(n):
-            t["a_grouped", n] = work.tile([P, P, PACK], BF16, name="a_grouped", align_bytes=64)
-            nc.scalar.copy(out=t["a_grouped", n][:], in_=t["attn_t", n][:].rearrange("p x m -> p m x"))
+            b, g, j = place(n)
+            if j == 0:
+                t["a_grouped", b, g] = work.tile([P, GROUP * P, PACK], BF16, name="a_grouped", align_bytes=64)
+            nc.scalar.copy(
+                out=t["a_grouped", b, g][:, j * P : (j + 1) * P, :],
+                in_=t["attn_t", n][:].rearrange("p x m -> p m x"),
+            )
 
         def attn_quantise(n):
-            t["a_mx", n] = quantise(work, "a", P, t["a_grouped", n][:].rearrange("p m x -> p (m x)"))
-
-        def context_matmuls(n):
             b, g, j = place(n)
-            a_codes, a_scales = t["a_mx", n]
+            if j == GROUP - 1:
+                grouped = t["a_grouped", b, g][:].rearrange("p m x -> p (m x)")
+                t["a_mx", b, g] = quantise(work, "a", GROUP * P, grouped)
+
+        def context_matmul(n):
+            b, g, j = place(n)
+            a_codes, a_scales = t["a_mx", b, g]
             v_codes, v_scales = v_mx[b]
-            t["ctx_ps", n] = psum.tile([P, D // P, P], F32, name="ctx_ps")
-            for f in range(D // P):
-                cols = slice(f * P, (f + 1) * P)
-                nc.tensor.matmul_mx(
-                    out=t["ctx_ps", n][:, f, :],
-                    lhsT=v_codes[:, cols].bitcast(FP8X4),
-                    lhsT_scale=v_scales[:, cols],
-                    rhs=a_codes[:].bitcast(FP8X4),
-                    rhs_scale=a_scales[:],
-                    start=True,
-                    stop=True,
-                )
+            cols = slice(j * P, (j + 1) * P)
+            t["ctx_ps", n] = psum.tile([P, GROUP * P], F32, name="ctx_ps")
+            nc.tensor.matmul_mx(
+                out=t["ctx_ps", n][:],
+                lhsT=v_codes[:, cols].bitcast(FP8X4),
+                lhsT_scale=v_scales[:, cols],
+                rhs=a_codes[:].bitcast(FP8X4),
+                rhs_scale=a_scales[:],
+                start=True,
+                stop=True,
+            )
 
         def context_out(n):
             b, g, j = place(n)
             if j == 0:
                 t["ctx_sb", b, g] = results.tile([P, D // P, GROUP * P], F32, name="ctx_sb")
             ctx_sb = t["ctx_sb", b, g]
-            nc.scalar.copy(out=ctx_sb[:, :, j * P : (j + 1) * P], in_=t["ctx_ps", n][:])
-            if j == GROUP - 1:
-                rows = out_0[b].rearrange("(f p g) n -> g p f n", p=P, g=TILES_PER_BATCH // GROUP)
-                nc.sync.dma_start(out=rows[g], in_=ctx_sb[:])
+            copy = nc.scalar.copy if j % 2 == 0 else nc.vector.tensor_copy
+            copy(out=ctx_sb[:, j, :], in_=t["ctx_ps", n][:])
+            rows = out_0[b].rearrange("(f p g) n -> g f p n", p=P, g=TILES_PER_BATCH // GROUP)
+            nc.sync.dma_start(out=rows[g, j], in_=ctx_sb[:, j, :])
 
         def run(stage, n):
             if 0 <= n < N_TILES:
                 stage(n)
 
-        for step in range(-4, N_TILES + 6):
-            run(context_matmuls, step - 5)
+        for step in range(-7, N_TILES + CONTEXT_LAG + 1):
+            run(context_matmul, step - CONTEXT_LAG)
             run(scores, step + 1)
             run(attn_transposes, step - 3)
-            run(q_transposes, step + 4)
+            run(q_transposes, step + 7)
             run(normalise, step - 2)
             run(add_and_max, step)
             run(exponent, step - 1)
-            run(context_out, step - 5)
+            run(context_out, step - CONTEXT_LAG)
             run(attn_regroup, step - 3)
             run(attn_quantise, step - 4)
-            run(q_regroup, step + 3)
-            run(q_quantise, step + 2)
+            run(q_regroup, step + 6)
+            run(q_quantise, step + 5)

@@ -146,15 +146,16 @@ def tile_multiheadattention_tupe_pb_t_kernel(tc, q, k, v, pos_bias, out_0, out_1
             k_codes, k_scales = k_mx[b]
             cols = slice(j * P, (j + 1) * P)
             t["score_ps", n] = psum.tile([P, SK], F32, name="score_ps")
-            nc.tensor.matmul_mx(
-                out=t["score_ps", n][:],
-                lhsT=q_codes[:, cols].bitcast(FP8X4),
-                lhsT_scale=q_scales[:, cols],
-                rhs=k_codes[:].bitcast(FP8X4),
-                rhs_scale=k_scales[:],
-                start=True,
-                stop=True,
-            )
+            for repeat in range(2):
+                nc.tensor.matmul_mx(
+                    out=t["score_ps", n][:],
+                    lhsT=q_codes[:, cols].bitcast(FP8X4),
+                    lhsT_scale=q_scales[:, cols],
+                    rhs=k_codes[:].bitcast(FP8X4),
+                    rhs_scale=k_scales[:],
+                    start=True,
+                    stop=True,
+                )
 
         def add_and_max(n):
             b, g, j = place(n)

@@ -146,16 +146,15 @@ def tile_multiheadattention_tupe_pb_t_kernel(tc, q, k, v, pos_bias, out_0, out_1
             k_codes, k_scales = k_mx[b]
             cols = slice(j * P, (j + 1) * P)
             t["score_ps", n] = psum.tile([P, SK], F32, name="score_ps")
-            for repeat in range(2):
-                nc.tensor.matmul_mx(
-                    out=t["score_ps", n][:],
-                    lhsT=q_codes[:, cols].bitcast(FP8X4),
-                    lhsT_scale=q_scales[:, cols],
-                    rhs=k_codes[:].bitcast(FP8X4),
-                    rhs_scale=k_scales[:],
-                    start=True,
-                    stop=True,
-                )
+            nc.tensor.matmul_mx(
+                out=t["score_ps", n][:],
+                lhsT=q_codes[:, cols].bitcast(FP8X4),
+                lhsT_scale=q_scales[:, cols],
+                rhs=k_codes[:].bitcast(FP8X4),
+                rhs_scale=k_scales[:],
+                start=True,
+                stop=True,
+            )
 
         def add_and_max(n):
             b, g, j = place(n)
@@ -189,7 +188,8 @@ def tile_multiheadattention_tupe_pb_t_kernel(tc, q, k, v, pos_bias, out_0, out_1
             attn_sb = t["attn_sb", b, g]
             inv_sum = work.tile([P, 1], F32, name="inv_sum")
             nc.vector.reciprocal(out=inv_sum[:], in_=t["row_sum", n][:])
-            nc.gpsimd.tensor_scalar(
+            multiply = nc.gpsimd.tensor_scalar if j % 2 == 0 else nc.vector.tensor_scalar
+            multiply(
                 out=attn_sb[:, j, :], in0=t["e_sb", n][:],
                 scalar1=inv_sum[:], scalar2=0.0, op0=ALU.mult, op1=ALU.add,
             )

@@ -20,7 +20,7 @@ GROUP = 4
 HALF = 2 * P * PACK
 TILES_PER_BATCH = SQ // P
 N_TILES = B * TILES_PER_BATCH
-CONTEXT_LAG = 12
+CONTEXT_LAG = 14
 INV_SCALE = 1.0 / math.sqrt(2.0 * 64.0)
 
 FLOPS = 2 * (2 * B * SQ * SK * D)
@@ -33,6 +33,7 @@ def tile_multiheadattention_tupe_pb_t_kernel(tc, q, k, v, pos_bias, out_0, out_1
         inputs = ctx.enter_context(tc.tile_pool(name="inputs", bufs=1))
         keep = ctx.enter_context(tc.tile_pool(name="keep", bufs=1))
         work = ctx.enter_context(tc.tile_pool(name="work", bufs=4))
+        soft = ctx.enter_context(tc.tile_pool(name="soft", bufs=6))
         results = ctx.enter_context(tc.tile_pool(name="results", bufs=3))
         psum = ctx.enter_context(tc.psum_pool(name="psum", bufs=2))
 
@@ -156,17 +157,19 @@ def tile_multiheadattention_tupe_pb_t_kernel(tc, q, k, v, pos_bias, out_0, out_1
                 stop=True,
             )
 
-        def add_and_max(n):
+        def add_pos(n):
             b, g, j = place(n)
             if n % TILES_PER_BATCH == 0:
                 prepare_v(b)
-            t["s_sb", n] = work.tile([P, SK], F32, name="s_sb")
-            row_max = work.tile([P, 1], F32, name="row_max")
-            t["exp_bias", n] = work.tile([P, 1], F32, name="exp_bias")
+            t["s_sb", n] = soft.tile([P, SK], F32, name="s_sb")
             nc.vector.tensor_tensor(
                 out=t["s_sb", n][:], in0=t["score_ps", n][:],
                 in1=pos_sb[g][:, j * SK : (j + 1) * SK], op=ALU.add,
             )
+
+        def row_maximum(n):
+            row_max = soft.tile([P, 1], F32, name="row_max")
+            t["exp_bias", n] = soft.tile([P, 1], F32, name="exp_bias")
             nc.vector.tensor_reduce(out=row_max[:], in_=t["s_sb", n][:], axis=AXIS_X, op=ALU.max)
             nc.gpsimd.tensor_scalar(
                 out=t["exp_bias", n][:], in0=row_max[:],
@@ -174,20 +177,23 @@ def tile_multiheadattention_tupe_pb_t_kernel(tc, q, k, v, pos_bias, out_0, out_1
             )
 
         def exponent(n):
-            t["e_sb", n] = work.tile([P, SK], F32, name="e_sb")
-            t["row_sum", n] = work.tile([P, 1], F32, name="row_sum")
+            t["e_sb", n] = soft.tile([P, SK], F32, name="e_sb")
+            t["row_sum", n] = soft.tile([P, 1], F32, name="row_sum")
             nc.scalar.activation(
                 out=t["e_sb", n][:], in_=t["s_sb", n][:], func=EXP,
                 bias=t["exp_bias", n][:], scale=INV_SCALE, accum_out=t["row_sum", n][:],
             )
+
+        def reciprocal(n):
+            t["inv_sum", n] = soft.tile([P, 1], F32, name="inv_sum")
+            nc.vector.reciprocal(out=t["inv_sum", n][:], in_=t["row_sum", n][:])
 
         def normalise(n):
             b, g, j = place(n)
             if j == 0:
                 t["attn_sb", b, g] = results.tile([P, GROUP, SK], F32, name="attn_sb")
             attn_sb = t["attn_sb", b, g]
-            inv_sum = work.tile([P, 1], F32, name="inv_sum")
-            nc.vector.reciprocal(out=inv_sum[:], in_=t["row_sum", n][:])
+            inv_sum = t["inv_sum", n]
             multiply = nc.gpsimd.tensor_scalar if j % 2 == 0 else nc.vector.tensor_scalar
             multiply(
                 out=attn_sb[:, j, :], in0=t["e_sb", n][:],
@@ -242,7 +248,7 @@ def tile_multiheadattention_tupe_pb_t_kernel(tc, q, k, v, pos_bias, out_0, out_1
             if j == 0:
                 t["ctx_sb", b, g] = results.tile([P, D // P, GROUP * P], F32, name="ctx_sb")
             ctx_sb = t["ctx_sb", b, g]
-            copy = nc.scalar.copy if j % 2 == 0 else nc.vector.tensor_copy
+            copy = nc.vector.tensor_copy if j == GROUP - 1 else nc.scalar.copy
             copy(out=ctx_sb[:, j, :], in_=t["ctx_ps", n][:])
             rows = out_0[b].rearrange("(f p g) n -> g f p n", p=P, g=TILES_PER_BATCH // GROUP)
             nc.sync.dma_start(out=rows[g, j], in_=ctx_sb[:, j, :])
@@ -254,13 +260,15 @@ def tile_multiheadattention_tupe_pb_t_kernel(tc, q, k, v, pos_bias, out_0, out_1
         for step in range(-7, N_TILES + CONTEXT_LAG + 1):
             run(context_matmul, step - CONTEXT_LAG)
             run(scores, step + 1)
-            run(attn_transposes, step - 3)
+            run(attn_transposes, step - 5)
             run(q_transposes, step + 7)
-            run(normalise, step - 2)
-            run(add_and_max, step)
-            run(exponent, step - 1)
+            run(reciprocal, step - 3)
+            run(add_pos, step)
+            run(row_maximum, step - 1)
+            run(normalise, step - 3)
+            run(exponent, step - 2)
             run(context_out, step - CONTEXT_LAG)
-            run(attn_regroup, step - 3)
-            run(attn_quantise, step - 4)
+            run(attn_regroup, step - 5)
+            run(attn_quantise, step - 6)
             run(q_regroup, step + 6)
             run(q_quantise, step + 5)

@@ -52,11 +52,15 @@ def tile_multiheadattention_tupe_pb_t_kernel(tc, q, k, v, pos_bias, out_0, out_1
                 in_=rows.rearrange("(j p) d -> p j d", p=P),
             )
 
+        def load_queries(table, key, rows, name):
+            table[key] = inputs.tile([P, GROUP * 512], BF16, name=name)
+            nc.sync.dma_start(out=table[key][:], in_=rows.rearrange("(p j) d -> p (j d)", j=GROUP))
+
         def load_q(b, g):
-            load_rows(q_sb, (b, g), q[b, group_rows(g), :], "q_sb_%d_%d" % (b, g))
+            load_queries(q_sb, (b, g), q[b, group_rows(g), :], "q_sb_%d_%d" % (b, g))
 
         def load_pos(g):
-            load_rows(pos_sb, g, pos_bias[group_rows(g), :], "pos_sb_%d" % g)
+            load_queries(pos_sb, g, pos_bias[group_rows(g), :], "pos_sb_%d" % g)
 
         load_rows(k_sb, 0, k[0], "k_sb_0")
         load_q(0, 0)
@@ -201,7 +205,7 @@ def tile_multiheadattention_tupe_pb_t_kernel(tc, q, k, v, pos_bias, out_0, out_1
             )
             if j == GROUP - 1:
                 nc.sync.dma_start(
-                    out=out_1[b, group_rows(g), :].rearrange("(j p) n -> p j n", p=P), in_=attn_sb[:]
+                    out=out_1[b, group_rows(g), :].rearrange("(p j) n -> p j n", j=GROUP), in_=attn_sb[:]
                 )
 
         def attn_transposes(n):
@@ -249,7 +253,10 @@ def tile_multiheadattention_tupe_pb_t_kernel(tc, q, k, v, pos_bias, out_0, out_1
                 t["ctx_sb", b, g] = results.tile([P, D // P, GROUP * P], F32, name="ctx_sb")
             ctx_sb = t["ctx_sb", b, g]
             copy = nc.vector.tensor_copy if j == GROUP - 1 else nc.scalar.copy
-            copy(out=ctx_sb[:, j, :], in_=t["ctx_ps", n][:])
+            copy(
+                out=ctx_sb[:, j, :].rearrange("p (m i) -> p m i", i=GROUP),
+                in_=t["ctx_ps", n][:].rearrange("p (i m) -> p m i", i=GROUP),
+            )
             rows = out_0[b].rearrange("(f p g) n -> g f p n", p=P, g=TILES_PER_BATCH // GROUP)
             nc.sync.dma_start(out=rows[g, j], in_=ctx_sb[:, j, :])
 

@@ -17,10 +17,10 @@ B, SQ, SK, D = 2, 2048, 512, 512
 P = 128
 PACK = 4
 GROUP = 4
-HALF = 2 * P * PACK
-TILES_PER_BATCH = SQ // P
-N_TILES = B * TILES_PER_BATCH
-CONTEXT_LAG = 14
+N_GROUPS = SQ // (GROUP * P)
+PAIR_COLS = 2 * P * PACK
+N_PAIRS = B * SQ // (2 * P)
+PAIRS_PER_BATCH = N_PAIRS // B
 INV_SCALE = 1.0 / math.sqrt(2.0 * 64.0)
 
 FLOPS = 2 * (2 * B * SQ * SK * D)
@@ -33,28 +33,23 @@ def tile_multiheadattention_tupe_pb_t_kernel(tc, q, k, v, pos_bias, out_0, out_1
         inputs = ctx.enter_context(tc.tile_pool(name="inputs", bufs=1))
         keep = ctx.enter_context(tc.tile_pool(name="keep", bufs=1))
         work = ctx.enter_context(tc.tile_pool(name="work", bufs=4))
-        soft = ctx.enter_context(tc.tile_pool(name="soft", bufs=6))
+        soft = ctx.enter_context(tc.tile_pool(name="soft", bufs=4))
         results = ctx.enter_context(tc.tile_pool(name="results", bufs=3))
         psum = ctx.enter_context(tc.psum_pool(name="psum", bufs=2))
-
-        def place(n):
-            return n // TILES_PER_BATCH, (n % TILES_PER_BATCH) // GROUP, n % GROUP
+        ctx.enter_context(tc.manual_schedule())
 
         def group_rows(g):
             return slice(g * GROUP * P, (g + 1) * GROUP * P)
 
         q_sb, pos_sb, k_sb, v_sb = {}, {}, {}, {}
 
-        def load_rows(table, key, rows, name):
+        def load_queries(table, key, rows, name, parts=1):
             table[key] = inputs.tile([P, GROUP * 512], BF16, name=name)
-            nc.sync.dma_start(
-                out=table[key][:].rearrange("p (j d) -> p j d", j=GROUP),
-                in_=rows.rearrange("(j p) d -> p j d", p=P),
-            )
-
-        def load_queries(table, key, rows, name):
-            table[key] = inputs.tile([P, GROUP * 512], BF16, name=name)
-            nc.sync.dma_start(out=table[key][:], in_=rows.rearrange("(p j) d -> p (j d)", j=GROUP))
+            cols = GROUP * 512 // parts
+            src = rows.rearrange("(p j) d -> p (j d)", j=GROUP)
+            for h in range(parts):
+                part = slice(h * cols, (h + 1) * cols)
+                nc.sync.dma_start(out=table[key][:, part], in_=src[:, part])
 
         def load_q(b, g):
             load_queries(q_sb, (b, g), q[b, group_rows(g), :], "q_sb_%d_%d" % (b, g))
@@ -62,19 +57,34 @@ def tile_multiheadattention_tupe_pb_t_kernel(tc, q, k, v, pos_bias, out_0, out_1
         def load_pos(g):
             load_queries(pos_sb, g, pos_bias[group_rows(g), :], "pos_sb_%d" % g)
 
-        load_rows(k_sb, 0, k[0], "k_sb_0")
+        def load_k(b):
+            k_sb[b] = inputs.tile([P, SK // P, D], BF16, name="k_sb_%d" % b)
+            for h in range(2):
+                nc.sync.dma_start(
+                    out=k_sb[b][:, 2 * h : 2 * h + 2, :],
+                    in_=k[b, h * 2 * P : (h + 1) * 2 * P, :].rearrange("(j p) d -> p j d", p=P),
+                )
+
+        def load_v(b):
+            v_sb[b] = inputs.tile([P, GROUP * D], BF16, name="v_sb_%d" % b)
+            nc.sync.dma_start(
+                out=v_sb[b][:].rearrange("p (u x) -> p u x", u=2),
+                in_=v[b].rearrange("(u p e) d -> p u (e d)", u=2, e=2),
+            )
+
+        load_k(0)
         load_q(0, 0)
-        load_q(0, 1)
         load_pos(0)
-        load_rows(v_sb, 0, v[0], "v_sb_0")
-        for g in range(2, TILES_PER_BATCH // GROUP):
-            load_q(0, g)
-            load_pos(g - 1)
-        load_pos(TILES_PER_BATCH // GROUP - 1)
-        load_rows(k_sb, 1, k[1], "k_sb_1")
-        load_q(1, 0)
-        load_rows(v_sb, 1, v[1], "v_sb_1")
-        for g in range(1, TILES_PER_BATCH // GROUP):
+        load_q(0, 1)
+        load_v(0)
+        load_v(1)
+        load_pos(1)
+        load_q(0, 2)
+        load_pos(2)
+        load_q(0, 3)
+        load_pos(3)
+        load_k(1)
+        for g in range(N_GROUPS):
             load_q(1, g)
 
         ident = const.tile([P, P], F32, name="ident")
@@ -84,11 +94,10 @@ def tile_multiheadattention_tupe_pb_t_kernel(tc, q, k, v, pos_bias, out_0, out_1
         nc.vector.memset(zero[:], 0.0)
         nc.scalar.activation(out=one[:], in_=zero[:], func=EXP)
 
-        def transpose_words(rows_sb, j, words_t):
-            words = rows_sb[:].bitcast(F32)
+        def transpose_words(rows, r, words_t):
+            words = rows.bitcast(F32)
             for u in range(2):
-                first = (2 * j + u) * P
-                nc.tensor.transpose(words_t[:, j % 2, u, :], words[:, first : first + P], ident[:])
+                nc.tensor.transpose(words_t[:, r, u, :], words[:, u * P : (u + 1) * P], ident[:])
 
         def regroup_words(copy, words_t, grouped):
             copy(
@@ -96,186 +105,234 @@ def tile_multiheadattention_tupe_pb_t_kernel(tc, q, k, v, pos_bias, out_0, out_1
                 in_=words_t[:].rearrange("p r u m -> p r m u"),
             )
 
-        def quantise(pool, name, width, grouped):
-            codes = pool.tile([P, width], U32, name=name + "_codes", align_bytes=64)
-            scales = pool.tile([P, width], U8, name=name + "_scales", align_bytes=64)
-            nc.vector.quantize_mx(out=codes[:].bitcast(FP8X4), scales=scales[:], in_=grouped)
-            return codes, scales
-
-        k_mx, v_mx = {}, {}
-
-        def prepare_k(b):
-            grouped = keep.tile([P, SK * PACK], BF16, name="k_grouped_%d" % b, align_bytes=64)
-            for h in range(2):
-                words_t = psum.tile([P, 2, 2, P], F32, name="words_t")
-                transpose_words(k_sb[b], 2 * h, words_t)
-                transpose_words(k_sb[b], 2 * h + 1, words_t)
-                copy = nc.vector.tensor_copy if h == 0 else nc.scalar.copy
-                regroup_words(copy, words_t, grouped[:, h * HALF : (h + 1) * HALF])
-            k_mx[b] = quantise(keep, "k%d" % b, SK, grouped[:])
-
-        def prepare_v(b):
-            grouped = keep.tile([P, D, PACK], BF16, name="v_grouped_%d" % b, align_bytes=64)
-            nc.vector.tensor_copy(out=grouped[:], in_=v_sb[b][:].rearrange("p (t d) -> p d t", t=PACK))
-            v_mx[b] = quantise(keep, "v%d" % b, D, grouped[:].rearrange("p d t -> p (d t)"))
+        def quantise(codes, scales, grouped):
+            nc.vector.quantize_mx(out=codes.bitcast(FP8X4), scales=scales, in_=grouped)
 
         t = {}
 
-        def q_transposes(n):
-            b, g, j = place(n)
-            if n % TILES_PER_BATCH == 0:
-                prepare_k(b)
-            if j % 2 == 0:
-                t["words_t", b, g, j // 2] = psum.tile([P, 2, 2, P], F32, name="words_t")
-            transpose_words(q_sb[(b, g)], j, t["words_t", b, g, j // 2])
+        def k_transposes(b, h):
+            t["k_words", b, h] = psum.tile([P, 2, 2, P], F32, name="words_t")
+            for r in range(2):
+                transpose_words(k_sb[b][:, 2 * h + r, :], r, t["k_words", b, h])
 
-        def q_regroup(n):
-            b, g, j = place(n)
-            if j == 0:
-                t["q_grouped", b, g] = work.tile([P, GROUP * P * PACK], BF16, name="q_grouped", align_bytes=64)
-            if j % 2 == 1:
-                h = j // 2
-                regroup_words(
-                    nc.scalar.copy, t["words_t", b, g, h],
-                    t["q_grouped", b, g][:, h * HALF : (h + 1) * HALF],
+        def k_regroup(b, h, copy):
+            if h == 0:
+                t["k_grouped", b] = keep.tile([P, SK * PACK], BF16, name="k_grouped_%d" % b, align_bytes=64)
+            regroup_words(copy, t["k_words", b, h], t["k_grouped", b][:, h * PAIR_COLS : (h + 1) * PAIR_COLS])
+
+        def k_quantise(b):
+            codes = keep.tile([P, SK], U32, name="k_codes_%d" % b, align_bytes=64)
+            scales = keep.tile([P, SK], U8, name="k_scales_%d" % b, align_bytes=64)
+            quantise(codes[:], scales[:], t["k_grouped", b][:])
+            t["k_mx", b] = codes, scales
+
+        def v_regroup(b, c):
+            if c == 0:
+                t["v_grouped", b] = keep.tile([P, D, PACK], BF16, name="v_grouped_%d" % b, align_bytes=64)
+            cols = slice(c * P, (c + 1) * P)
+            nc.gpsimd.tensor_scalar(
+                out=t["v_grouped", b][:, cols, :],
+                in0=v_sb[b][:].rearrange("p (t d) -> p d t", t=PACK)[:, cols, :],
+                scalar1=1.0, scalar2=0.0, op0=ALU.mult, op1=ALU.add,
+            )
+
+        def v_quantise(b):
+            codes = keep.tile([P, D], U32, name="v_codes_%d" % b, align_bytes=64)
+            scales = keep.tile([P, D], U8, name="v_scales_%d" % b, align_bytes=64)
+            quantise(codes[:], scales[:], t["v_grouped", b][:].rearrange("p d t -> p (d t)"))
+            t["v_mx", b] = codes, scales
+
+        def place(i):
+            return i // PAIRS_PER_BATCH, (i % PAIRS_PER_BATCH) // 2, i % 2
+
+        def q_transposes(i):
+            b, g, h = place(i)
+            t["q_words", i] = psum.tile([P, 2, 2, P], F32, name="words_t")
+            for r in range(2):
+                j = 2 * h + r
+                transpose_words(q_sb[b, g][:, j * D : (j + 1) * D], r, t["q_words", i])
+
+        def q_regroup(i):
+            t["q_grouped", i] = work.tile([P, PAIR_COLS], BF16, name="q_grouped", align_bytes=64)
+            regroup_words(nc.scalar.copy, t["q_words", i], t["q_grouped", i][:])
+
+        def q_quantise(i):
+            codes = work.tile([P, 2 * P], U32, name="q_codes", align_bytes=64)
+            scales = work.tile([P, 2 * P], U8, name="q_scales", align_bytes=64)
+            quantise(codes[:], scales[:], t["q_grouped", i][:])
+            t["q_mx", i] = codes, scales
+
+        def scores(i):
+            b = place(i)[0]
+            q_codes, q_scales = t["q_mx", i]
+            k_codes, k_scales = t["k_mx", b]
+            for r in range(2):
+                cols = slice(r * P, (r + 1) * P)
+                t["score_ps", i, r] = psum.tile([P, SK], F32, name="score_ps")
+                nc.tensor.matmul_mx(
+                    out=t["score_ps", i, r][:],
+                    lhsT=q_codes[:, cols].bitcast(FP8X4),
+                    lhsT_scale=q_scales[:, cols],
+                    rhs=k_codes[:].bitcast(FP8X4),
+                    rhs_scale=k_scales[:],
+                    start=True,
+                    stop=True,
                 )
 
-        def q_quantise(n):
-            b, g, j = place(n)
-            if j == GROUP - 1:
-                t["q_mx", b, g] = quantise(work, "q", GROUP * P, t["q_grouped", b, g][:])
+        def add_pos(i):
+            g, h = place(i)[1:]
+            t["s_sb", i] = soft.tile([P, 2, SK], F32, name="s_sb")
+            for r in range(2):
+                j = 2 * h + r
+                nc.vector.tensor_tensor(
+                    out=t["s_sb", i][:, r, :], in0=t["score_ps", i, r][:],
+                    in1=pos_sb[g][:, j * SK : (j + 1) * SK], op=ALU.add,
+                )
 
-        def scores(n):
-            b, g, j = place(n)
-            q_codes, q_scales = t["q_mx", b, g]
-            k_codes, k_scales = k_mx[b]
-            cols = slice(j * P, (j + 1) * P)
-            t["score_ps", n] = psum.tile([P, SK], F32, name="score_ps")
-            nc.tensor.matmul_mx(
-                out=t["score_ps", n][:],
-                lhsT=q_codes[:, cols].bitcast(FP8X4),
-                lhsT_scale=q_scales[:, cols],
-                rhs=k_codes[:].bitcast(FP8X4),
-                rhs_scale=k_scales[:],
-                start=True,
-                stop=True,
-            )
+        def row_maximum(i):
+            t["row_max", i] = soft.tile([P, 2], F32, name="row_max")
+            nc.vector.tensor_reduce(out=t["row_max", i][:], in_=t["s_sb", i][:], axis=AXIS_X, op=ALU.max)
 
-        def add_pos(n):
-            b, g, j = place(n)
-            if n % TILES_PER_BATCH == 0:
-                prepare_v(b)
-            t["s_sb", n] = soft.tile([P, SK], F32, name="s_sb")
-            nc.vector.tensor_tensor(
-                out=t["s_sb", n][:], in0=t["score_ps", n][:],
-                in1=pos_sb[g][:, j * SK : (j + 1) * SK], op=ALU.add,
-            )
-
-        def row_maximum(n):
-            row_max = soft.tile([P, 1], F32, name="row_max")
-            t["exp_bias", n] = soft.tile([P, 1], F32, name="exp_bias")
-            nc.vector.tensor_reduce(out=row_max[:], in_=t["s_sb", n][:], axis=AXIS_X, op=ALU.max)
+        def exp_bias(i):
+            t["exp_bias", i] = soft.tile([P, 2], F32, name="exp_bias")
             nc.gpsimd.tensor_scalar(
-                out=t["exp_bias", n][:], in0=row_max[:],
+                out=t["exp_bias", i][:], in0=t["row_max", i][:],
                 scalar1=-INV_SCALE, scalar2=0.0, op0=ALU.mult, op1=ALU.add,
             )
 
-        def exponent(n):
-            t["e_sb", n] = soft.tile([P, SK], F32, name="e_sb")
-            t["row_sum", n] = soft.tile([P, 1], F32, name="row_sum")
-            nc.scalar.activation(
-                out=t["e_sb", n][:], in_=t["s_sb", n][:], func=EXP,
-                bias=t["exp_bias", n][:], scale=INV_SCALE, accum_out=t["row_sum", n][:],
-            )
+        def exponent(i):
+            t["e_sb", i] = soft.tile([P, 2, SK], F32, name="e_sb")
+            t["row_sum", i] = soft.tile([P, 2], F32, name="row_sum")
+            for r in range(2):
+                nc.scalar.activation(
+                    out=t["e_sb", i][:, r, :], in_=t["s_sb", i][:, r, :], func=EXP,
+                    bias=t["exp_bias", i][:, r : r + 1], scale=INV_SCALE,
+                    accum_out=t["row_sum", i][:, r : r + 1],
+                )
 
-        def reciprocal(n):
-            t["inv_sum", n] = soft.tile([P, 1], F32, name="inv_sum")
-            nc.vector.reciprocal(out=t["inv_sum", n][:], in_=t["row_sum", n][:])
+        def reciprocal(i):
+            t["inv_sum", i] = soft.tile([P, 2], F32, name="inv_sum")
+            nc.vector.reciprocal(out=t["inv_sum", i][:], in_=t["row_sum", i][:])
 
-        def normalise(n):
-            b, g, j = place(n)
-            if j == 0:
-                t["attn_sb", b, g] = results.tile([P, GROUP, SK], F32, name="attn_sb")
-            attn_sb = t["attn_sb", b, g]
-            inv_sum = t["inv_sum", n]
-            multiply = nc.gpsimd.tensor_scalar if j % 2 == 0 else nc.vector.tensor_scalar
+        def normalise(multiply, out, i, r):
             multiply(
-                out=attn_sb[:, j, :], in0=t["e_sb", n][:],
-                scalar1=inv_sum[:], scalar2=0.0, op0=ALU.mult, op1=ALU.add,
+                out=out, in0=t["e_sb", i][:, r, :],
+                scalar1=t["inv_sum", i][:, r : r + 1], scalar2=0.0, op0=ALU.mult, op1=ALU.add,
             )
-            if j == GROUP - 1:
+
+        def attn_rounded(i):
+            t["a_bf", i] = soft.tile([P, 2, SK], BF16, name="a_bf")
+            for r in range(2):
+                normalise(nc.vector.tensor_scalar, t["a_bf", i][:, r, :], i, r)
+
+        def attn_out(i):
+            b, g, h = place(i)
+            if h == 0:
+                t["attn_sb", b, g] = results.tile([P, GROUP, SK], F32, name="attn_sb")
+            for r in range(2):
+                normalise(nc.gpsimd.tensor_scalar, t["attn_sb", b, g][:, 2 * h + r, :], i, r)
+            if h == 1:
                 nc.sync.dma_start(
-                    out=out_1[b, group_rows(g), :].rearrange("(p j) n -> p j n", j=GROUP), in_=attn_sb[:]
+                    out=out_1[b, group_rows(g), :].rearrange("(p j) n -> p j n", j=GROUP),
+                    in_=t["attn_sb", b, g][:],
                 )
 
-        def attn_transposes(n):
-            b, g, j = place(n)
-            t["attn_t", n] = psum.tile([P, PACK, P], F32, name="attn_t")
-            for x in range(PACK):
-                nc.tensor.transpose(
-                    t["attn_t", n][:, x, :], t["attn_sb", b, g][:, j, x * P : (x + 1) * P], ident[:]
-                )
+        def attn_transposes(i):
+            t["a_words", i] = psum.tile([P, 2, 2, P], F32, name="attn_t")
+            for r in range(2):
+                transpose_words(t["a_bf", i][:, r, :], r, t["a_words", i])
 
-        def attn_regroup(n):
-            b, g, j = place(n)
-            if j == 0:
-                t["a_grouped", b, g] = work.tile([P, GROUP * P, PACK], BF16, name="a_grouped", align_bytes=64)
-            nc.scalar.copy(
-                out=t["a_grouped", b, g][:, j * P : (j + 1) * P, :],
-                in_=t["attn_t", n][:].rearrange("p x m -> p m x"),
-            )
+        def attn_regroup(i):
+            t["a_grouped", i] = work.tile([P, PAIR_COLS], BF16, name="a_grouped", align_bytes=64)
+            regroup_words(nc.scalar.copy, t["a_words", i], t["a_grouped", i][:])
 
-        def attn_quantise(n):
-            b, g, j = place(n)
-            if j == GROUP - 1:
-                grouped = t["a_grouped", b, g][:].rearrange("p m x -> p (m x)")
-                t["a_mx", b, g] = quantise(work, "a", GROUP * P, grouped)
+        def attn_quantise(i):
+            b, g, h = place(i)
+            if h == 0:
+                codes = work.tile([P, GROUP * P], U32, name="a_codes", align_bytes=64)
+                scales = work.tile([P, GROUP * P], U8, name="a_scales", align_bytes=64)
+                t["a_mx", b, g] = codes, scales
+            codes, scales = t["a_mx", b, g]
+            cols = slice(h * 2 * P, (h + 1) * 2 * P)
+            quantise(codes[:, cols], scales[:, cols], t["a_grouped", i][:])
 
-        def context_matmul(n):
-            b, g, j = place(n)
+        def context_matmul(i):
+            b, g, h = place(i)
             a_codes, a_scales = t["a_mx", b, g]
-            v_codes, v_scales = v_mx[b]
-            cols = slice(j * P, (j + 1) * P)
-            t["ctx_ps", n] = psum.tile([P, GROUP * P], F32, name="ctx_ps")
-            nc.tensor.matmul_mx(
-                out=t["ctx_ps", n][:],
-                lhsT=v_codes[:, cols].bitcast(FP8X4),
-                lhsT_scale=v_scales[:, cols],
-                rhs=a_codes[:].bitcast(FP8X4),
-                rhs_scale=a_scales[:],
-                start=True,
-                stop=True,
-            )
+            v_codes, v_scales = t["v_mx", b]
+            for f in (2 * h, 2 * h + 1):
+                cols = slice(f * P, (f + 1) * P)
+                t["ctx_ps", b, g, f] = psum.tile([P, GROUP * P], F32, name="ctx_ps")
+                nc.tensor.matmul_mx(
+                    out=t["ctx_ps", b, g, f][:],
+                    lhsT=v_codes[:, cols].bitcast(FP8X4),
+                    lhsT_scale=v_scales[:, cols],
+                    rhs=a_codes[:].bitcast(FP8X4),
+                    rhs_scale=a_scales[:],
+                    start=True,
+                    stop=True,
+                )
 
-        def context_out(n):
-            b, g, j = place(n)
-            if j == 0:
+        def context_out(i, copies):
+            b, g, h = place(i)
+            if h == 0:
                 t["ctx_sb", b, g] = results.tile([P, D // P, GROUP * P], F32, name="ctx_sb")
             ctx_sb = t["ctx_sb", b, g]
-            copy = nc.vector.tensor_copy if j == GROUP - 1 else nc.scalar.copy
-            copy(
-                out=ctx_sb[:, j, :].rearrange("p (m i) -> p m i", i=GROUP),
-                in_=t["ctx_ps", n][:].rearrange("p (i m) -> p m i", i=GROUP),
-            )
-            rows = out_0[b].rearrange("(f p g) n -> g f p n", p=P, g=TILES_PER_BATCH // GROUP)
-            nc.sync.dma_start(out=rows[g, j], in_=ctx_sb[:, j, :])
+            rows = out_0[b].rearrange("(f p g) n -> g f p n", p=P, g=N_GROUPS)
+            for f, copy in zip((2 * h, 2 * h + 1), copies):
+                copy(
+                    out=ctx_sb[:, f, :].rearrange("p (m j) -> p m j", j=GROUP),
+                    in_=t["ctx_ps", b, g, f][:].rearrange("p (j m) -> p m j", j=GROUP),
+                )
+                nc.sync.dma_start(out=rows[g, f], in_=ctx_sb[:, f, :])
 
-        def run(stage, n):
-            if 0 <= n < N_TILES:
-                stage(n)
+        def run(stage, i, *args):
+            if 0 <= i < N_PAIRS:
+                stage(i, *args)
 
-        for step in range(-7, N_TILES + CONTEXT_LAG + 1):
-            run(context_matmul, step - CONTEXT_LAG)
+        k_transposes(0, 0)
+        k_transposes(0, 1)
+        k_regroup(0, 0, nc.vector.tensor_copy)
+        k_regroup(0, 1, nc.scalar.copy)
+
+        for step in range(-3, N_PAIRS + 7):
+            both = (nc.scalar.copy, nc.scalar.copy) if step < N_PAIRS else (nc.scalar.copy, nc.vector.tensor_copy)
             run(scores, step + 1)
-            run(attn_transposes, step - 5)
-            run(q_transposes, step + 7)
-            run(reciprocal, step - 3)
+            run(q_transposes, step + 3)
+            if step in (3, 4):
+                k_transposes(1, step - 3)
+            run(reciprocal, step - 2)
+            run(attn_out, step - 2)
             run(add_pos, step)
-            run(row_maximum, step - 1)
-            run(normalise, step - 3)
-            run(exponent, step - 2)
-            run(context_out, step - CONTEXT_LAG)
-            run(attn_regroup, step - 5)
-            run(attn_quantise, step - 6)
-            run(q_regroup, step + 6)
-            run(q_quantise, step + 5)
+            run(attn_rounded, step - 2)
+            run(row_maximum, step)
+            if step == 0:
+                v_regroup(0, 0)
+                v_regroup(0, 1)
+            run(exp_bias, step)
+            if step == 0:
+                v_regroup(0, 2)
+                v_regroup(0, 3)
+                v_regroup(1, 0)
+                v_regroup(1, 1)
+            if step == 1:
+                v_regroup(1, 2)
+                v_regroup(1, 3)
+            run(attn_transposes, step - 2)
+            run(exponent, step - 1)
+            run(context_out, step - 6, both)
+            run(q_regroup, step + 3)
+            if step in (3, 4):
+                k_regroup(1, step - 3, nc.scalar.copy)
+            run(attn_regroup, step - 2)
+            if step == -2:
+                k_quantise(0)
+            if step == 5:
+                k_quantise(1)
+            if step == 3:
+                v_quantise(0)
+            if step == 4:
+                v_quantise(1)
+            run(q_quantise, step + 2)
+            run(attn_quantise, step - 3)
+            run(context_matmul, step - 5)

@@ -66,11 +66,8 @@ def tile_multiheadattention_tupe_pb_t_kernel(tc, q, k, v, pos_bias, out_0, out_1
                 )
 
         def load_v(b):
-            v_sb[b] = inputs.tile([P, GROUP * D], BF16, name="v_sb_%d" % b)
-            nc.sync.dma_start(
-                out=v_sb[b][:].rearrange("p (u x) -> p u x", u=2),
-                in_=v[b].rearrange("(u p e) d -> p u (e d)", u=2, e=2),
-            )
+            v_sb[b] = inputs.tile([P, PACK, D], BF16, name="v_sb_%d" % b)
+            nc.sync.dma_start(out=v_sb[b][:], in_=v[b].rearrange("(t p) d -> p t d", p=P))
 
         load_k(0)
         load_q(0, 0)
@@ -132,7 +129,7 @@ def tile_multiheadattention_tupe_pb_t_kernel(tc, q, k, v, pos_bias, out_0, out_1
             cols = slice(c * P, (c + 1) * P)
             nc.gpsimd.tensor_scalar(
                 out=t["v_grouped", b][:, cols, :],
-                in0=v_sb[b][:].rearrange("p (t d) -> p d t", t=PACK)[:, cols, :],
+                in0=v_sb[b][:].rearrange("p t d -> p d t")[:, cols, :],
                 scalar1=1.0, scalar2=0.0, op0=ALU.mult, op1=ALU.add,
             )
 
@@ -152,22 +149,30 @@ def tile_multiheadattention_tupe_pb_t_kernel(tc, q, k, v, pos_bias, out_0, out_1
                 j = 2 * h + r
                 transpose_words(q_sb[b, g][:, j * D : (j + 1) * D], r, t["q_words", i])
 
+        def quantise_group(name, source, i):
+            b, g, h = place(i)
+            if h == 1:
+                codes = work.tile([P, GROUP * P], U32, name=name + "_codes", align_bytes=64)
+                scales = work.tile([P, GROUP * P], U8, name=name + "_scales", align_bytes=64)
+                quantise(codes[:], scales[:], t[source, b, g][:])
+                t[name, b, g] = codes, scales
+
         def q_regroup(i):
-            t["q_grouped", i] = work.tile([P, PAIR_COLS], BF16, name="q_grouped", align_bytes=64)
-            regroup_words(nc.scalar.copy, t["q_words", i], t["q_grouped", i][:])
+            b, g, h = place(i)
+            if h == 0:
+                t["q_grouped", b, g] = work.tile([P, 2 * PAIR_COLS], BF16, name="q_grouped", align_bytes=64)
+            grouped = t["q_grouped", b, g][:, h * PAIR_COLS : (h + 1) * PAIR_COLS]
+            regroup_words(nc.scalar.copy, t["q_words", i], grouped)
 
         def q_quantise(i):
-            codes = work.tile([P, 2 * P], U32, name="q_codes", align_bytes=64)
-            scales = work.tile([P, 2 * P], U8, name="q_scales", align_bytes=64)
-            quantise(codes[:], scales[:], t["q_grouped", i][:])
-            t["q_mx", i] = codes, scales
+            quantise_group("q_mx", "q_grouped", i)
 
         def scores(i):
-            b = place(i)[0]
-            q_codes, q_scales = t["q_mx", i]
+            b, g, h = place(i)
+            q_codes, q_scales = t["q_mx", b, g]
             k_codes, k_scales = t["k_mx", b]
             for r in range(2):
-                cols = slice(r * P, (r + 1) * P)
+                cols = slice((2 * h + r) * P, (2 * h + r + 1) * P)
                 t["score_ps", i, r] = psum.tile([P, SK], F32, name="score_ps")
                 nc.tensor.matmul_mx(
                     out=t["score_ps", i, r][:],
@@ -214,23 +219,15 @@ def tile_multiheadattention_tupe_pb_t_kernel(tc, q, k, v, pos_bias, out_0, out_1
             t["inv_sum", i] = soft.tile([P, 2], F32, name="inv_sum")
             nc.vector.reciprocal(out=t["inv_sum", i][:], in_=t["row_sum", i][:])
 
-        def normalise(multiply, out, i, r):
-            multiply(
-                out=out, in0=t["e_sb", i][:, r, :],
-                scalar1=t["inv_sum", i][:, r : r + 1], scalar2=0.0, op0=ALU.mult, op1=ALU.add,
-            )
-
-        def attn_rounded(i):
-            t["a_bf", i] = soft.tile([P, 2, SK], BF16, name="a_bf")
-            for r in range(2):
-                normalise(nc.vector.tensor_scalar, t["a_bf", i][:, r, :], i, r)
-
-        def attn_out(i):
+        def normalise(i):
             b, g, h = place(i)
             if h == 0:
                 t["attn_sb", b, g] = results.tile([P, GROUP, SK], F32, name="attn_sb")
             for r in range(2):
-                normalise(nc.gpsimd.tensor_scalar, t["attn_sb", b, g][:, 2 * h + r, :], i, r)
+                nc.vector.tensor_scalar(
+                    out=t["attn_sb", b, g][:, 2 * h + r, :], in0=t["e_sb", i][:, r, :],
+                    scalar1=t["inv_sum", i][:, r : r + 1], scalar2=0.0, op0=ALU.mult, op1=ALU.add,
+                )
             if h == 1:
                 nc.sync.dma_start(
                     out=out_1[b, group_rows(g), :].rearrange("(p j) n -> p j n", j=GROUP),
@@ -238,23 +235,29 @@ def tile_multiheadattention_tupe_pb_t_kernel(tc, q, k, v, pos_bias, out_0, out_1
                 )
 
         def attn_transposes(i):
-            t["a_words", i] = psum.tile([P, 2, 2, P], F32, name="attn_t")
+            b, g, h = place(i)
             for r in range(2):
-                transpose_words(t["a_bf", i][:, r, :], r, t["a_words", i])
+                t["attn_t", i, r] = psum.tile([P, PACK, P], F32, name="attn_t")
+                for x in range(PACK):
+                    nc.tensor.transpose(
+                        t["attn_t", i, r][:, x, :],
+                        t["attn_sb", b, g][:, 2 * h + r, x * P : (x + 1) * P],
+                        ident[:],
+                    )
 
         def attn_regroup(i):
-            t["a_grouped", i] = work.tile([P, PAIR_COLS], BF16, name="a_grouped", align_bytes=64)
-            regroup_words(nc.scalar.copy, t["a_words", i], t["a_grouped", i][:])
-
-        def attn_quantise(i):
             b, g, h = place(i)
             if h == 0:
-                codes = work.tile([P, GROUP * P], U32, name="a_codes", align_bytes=64)
-                scales = work.tile([P, GROUP * P], U8, name="a_scales", align_bytes=64)
-                t["a_mx", b, g] = codes, scales
-            codes, scales = t["a_mx", b, g]
-            cols = slice(h * 2 * P, (h + 1) * 2 * P)
-            quantise(codes[:, cols], scales[:, cols], t["a_grouped", i][:])
+                t["a_grouped", b, g] = work.tile([P, 2 * PAIR_COLS], BF16, name="a_grouped", align_bytes=64)
+            grouped = t["a_grouped", b, g][:].rearrange("p (j m x) -> p j m x", j=GROUP, x=PACK)
+            for r in range(2):
+                nc.scalar.copy(
+                    out=grouped[:, 2 * h + r],
+                    in_=t["attn_t", i, r][:].rearrange("p x m -> p m x"),
+                )
+
+        def attn_quantise(i):
+            quantise_group("a_mx", "a_grouped", i)
 
         def context_matmul(i):
             b, g, h = place(i)
@@ -273,13 +276,14 @@ def tile_multiheadattention_tupe_pb_t_kernel(tc, q, k, v, pos_bias, out_0, out_1
                     stop=True,
                 )
 
-        def context_out(i, copies):
+        def context_out(i, last):
             b, g, h = place(i)
             if h == 0:
                 t["ctx_sb", b, g] = results.tile([P, D // P, GROUP * P], F32, name="ctx_sb")
             ctx_sb = t["ctx_sb", b, g]
             rows = out_0[b].rearrange("(f p g) n -> g f p n", p=P, g=N_GROUPS)
-            for f, copy in zip((2 * h, 2 * h + 1), copies):
+            for f in (2 * h, 2 * h + 1):
+                copy = nc.vector.tensor_copy if f == 3 or (last and f == 1) else nc.scalar.copy
                 copy(
                     out=ctx_sb[:, f, :].rearrange("p (m j) -> p m j", j=GROUP),
                     in_=t["ctx_ps", b, g, f][:].rearrange("p (j m) -> p m j", j=GROUP),
@@ -295,16 +299,16 @@ def tile_multiheadattention_tupe_pb_t_kernel(tc, q, k, v, pos_bias, out_0, out_1
         k_regroup(0, 0, nc.vector.tensor_copy)
         k_regroup(0, 1, nc.scalar.copy)
 
-        for step in range(-3, N_PAIRS + 7):
-            both = (nc.scalar.copy, nc.scalar.copy) if step < N_PAIRS else (nc.scalar.copy, nc.vector.tensor_copy)
+        for step in range(-4, N_PAIRS + 7):
             run(scores, step + 1)
-            run(q_transposes, step + 3)
+            q_pairs = (step + 4,) if step not in (-2, -1) else (2, 3) if step == -1 else ()
+            for i in q_pairs:
+                run(q_transposes, i)
             if step in (3, 4):
                 k_transposes(1, step - 3)
             run(reciprocal, step - 2)
-            run(attn_out, step - 2)
             run(add_pos, step)
-            run(attn_rounded, step - 2)
+            run(normalise, step - 2)
             run(row_maximum, step)
             if step == 0:
                 v_regroup(0, 0)
@@ -320,8 +324,9 @@ def tile_multiheadattention_tupe_pb_t_kernel(tc, q, k, v, pos_bias, out_0, out_1
                 v_regroup(1, 3)
             run(attn_transposes, step - 2)
             run(exponent, step - 1)
-            run(context_out, step - 6, both)
-            run(q_regroup, step + 3)
+            run(context_out, step - 6, step >= N_PAIRS)
+            for i in q_pairs:
+                run(q_regroup, i)
             if step in (3, 4):
                 k_regroup(1, step - 3, nc.scalar.copy)
             run(attn_regroup, step - 2)
@@ -333,6 +338,6 @@ def tile_multiheadattention_tupe_pb_t_kernel(tc, q, k, v, pos_bias, out_0, out_1
                 v_quantise(0)
             if step == 4:
                 v_quantise(1)
-            run(q_quantise, step + 2)
+            run(q_quantise, step + 3)
             run(attn_quantise, step - 3)
             run(context_matmul, step - 5)

@@ -127,11 +127,7 @@ def tile_multiheadattention_tupe_pb_t_kernel(tc, q, k, v, pos_bias, out_0, out_1
             if c == 0:
                 t["v_grouped", b] = keep.tile([P, D, PACK], BF16, name="v_grouped_%d" % b, align_bytes=64)
             cols = slice(c * P, (c + 1) * P)
-            nc.gpsimd.tensor_scalar(
-                out=t["v_grouped", b][:, cols, :],
-                in0=v_sb[b][:].rearrange("p t d -> p d t")[:, cols, :],
-                scalar1=1.0, scalar2=0.0, op0=ALU.mult, op1=ALU.add,
-            )
+            nc.scalar.copy(out=t["v_grouped", b][:, cols, :], in_=v_sb[b][:].rearrange("p t d -> p d t")[:, cols, :])
 
         def v_quantise(b):
             codes = keep.tile([P, D], U32, name="v_codes_%d" % b, align_bytes=64)
@@ -144,7 +140,7 @@ def tile_multiheadattention_tupe_pb_t_kernel(tc, q, k, v, pos_bias, out_0, out_1
 
         def q_transposes(i):
             b, g, h = place(i)
-            t["q_words", i] = psum.tile([P, 2, 2, P], F32, name="words_t")
+            t["q_words", i] = psum.tile([P, 2, 2, P], F32, name="attn_t" if i < 2 else "words_t")
             for r in range(2):
                 j = 2 * h + r
                 transpose_words(q_sb[b, g][:, j * D : (j + 1) * D], r, t["q_words", i])
@@ -162,10 +158,19 @@ def tile_multiheadattention_tupe_pb_t_kernel(tc, q, k, v, pos_bias, out_0, out_1
             if h == 0:
                 t["q_grouped", b, g] = work.tile([P, 2 * PAIR_COLS], BF16, name="q_grouped", align_bytes=64)
             grouped = t["q_grouped", b, g][:, h * PAIR_COLS : (h + 1) * PAIR_COLS]
-            regroup_words(nc.scalar.copy, t["q_words", i], grouped)
+            regroup_words(nc.vector.tensor_copy if i == 0 else nc.scalar.copy, t["q_words", i], grouped)
 
         def q_quantise(i):
-            quantise_group("q_mx", "q_grouped", i)
+            if i >= 2:
+                quantise_group("q_mx", "q_grouped", i)
+                return
+            if i == 0:
+                codes = work.tile([P, GROUP * P], U32, name="q_mx_codes", align_bytes=64)
+                scales = work.tile([P, GROUP * P], U8, name="q_mx_scales", align_bytes=64)
+                t["q_mx", 0, 0] = codes, scales
+            codes, scales = t["q_mx", 0, 0]
+            cols = slice(i * 2 * P, (i + 1) * 2 * P)
+            quantise(codes[:, cols], scales[:, cols], t["q_grouped", 0, 0][:, i * PAIR_COLS : (i + 1) * PAIR_COLS])
 
         def scores(i):
             b, g, h = place(i)
@@ -196,7 +201,10 @@ def tile_multiheadattention_tupe_pb_t_kernel(tc, q, k, v, pos_bias, out_0, out_1
 
         def row_maximum(i):
             t["row_max", i] = soft.tile([P, 2], F32, name="row_max")
-            nc.vector.tensor_reduce(out=t["row_max", i][:], in_=t["s_sb", i][:], axis=AXIS_X, op=ALU.max)
+            for r in range(2):
+                nc.vector.tensor_reduce(
+                    out=t["row_max", i][:, r : r + 1], in_=t["s_sb", i][:, r, :], axis=AXIS_X, op=ALU.max
+                )
 
         def exp_bias(i):
             t["exp_bias", i] = soft.tile([P, 2], F32, name="exp_bias")
@@ -223,8 +231,9 @@ def tile_multiheadattention_tupe_pb_t_kernel(tc, q, k, v, pos_bias, out_0, out_1
             b, g, h = place(i)
             if h == 0:
                 t["attn_sb", b, g] = results.tile([P, GROUP, SK], F32, name="attn_sb")
+            multiply = nc.gpsimd.tensor_scalar if i < N_PAIRS - 2 else nc.vector.tensor_scalar
             for r in range(2):
-                nc.vector.tensor_scalar(
+                multiply(
                     out=t["attn_sb", b, g][:, 2 * h + r, :], in0=t["e_sb", i][:, r, :],
                     scalar1=t["inv_sum", i][:, r : r + 1], scalar2=0.0, op0=ALU.mult, op1=ALU.add,
                 )
@@ -251,7 +260,8 @@ def tile_multiheadattention_tupe_pb_t_kernel(tc, q, k, v, pos_bias, out_0, out_1
                 t["a_grouped", b, g] = work.tile([P, 2 * PAIR_COLS], BF16, name="a_grouped", align_bytes=64)
             grouped = t["a_grouped", b, g][:].rearrange("p (j m x) -> p j m x", j=GROUP, x=PACK)
             for r in range(2):
-                nc.scalar.copy(
+                copy = nc.vector.tensor_copy if i == N_PAIRS - 1 and r == 1 else nc.scalar.copy
+                copy(
                     out=grouped[:, 2 * h + r],
                     in_=t["attn_t", i, r][:].rearrange("p x m -> p m x"),
                 )
@@ -265,7 +275,8 @@ def tile_multiheadattention_tupe_pb_t_kernel(tc, q, k, v, pos_bias, out_0, out_1
             v_codes, v_scales = t["v_mx", b]
             for f in (2 * h, 2 * h + 1):
                 cols = slice(f * P, (f + 1) * P)
-                t["ctx_ps", b, g, f] = psum.tile([P, GROUP * P], F32, name="ctx_ps")
+                name = "score_ps" if i >= N_PAIRS - 4 and f % 2 == 1 else "ctx_ps"
+                t["ctx_ps", b, g, f] = psum.tile([P, GROUP * P], F32, name=name)
                 nc.tensor.matmul_mx(
                     out=t["ctx_ps", b, g, f][:],
                     lhsT=v_codes[:, cols].bitcast(FP8X4),
@@ -276,14 +287,14 @@ def tile_multiheadattention_tupe_pb_t_kernel(tc, q, k, v, pos_bias, out_0, out_1
                     stop=True,
                 )
 
-        def context_out(i, last):
+        def context_out(i):
             b, g, h = place(i)
             if h == 0:
                 t["ctx_sb", b, g] = results.tile([P, D // P, GROUP * P], F32, name="ctx_sb")
             ctx_sb = t["ctx_sb", b, g]
             rows = out_0[b].rearrange("(f p g) n -> g f p n", p=P, g=N_GROUPS)
             for f in (2 * h, 2 * h + 1):
-                copy = nc.vector.tensor_copy if f == 3 or (last and f == 1) else nc.scalar.copy
+                copy = nc.vector.tensor_copy if f % 2 == 1 else nc.scalar.copy
                 copy(
                     out=ctx_sb[:, f, :].rearrange("p (m j) -> p m j", j=GROUP),
                     in_=t["ctx_ps", b, g, f][:].rearrange("p (j m) -> p m j", j=GROUP),
@@ -296,12 +307,19 @@ def tile_multiheadattention_tupe_pb_t_kernel(tc, q, k, v, pos_bias, out_0, out_1
 
         k_transposes(0, 0)
         k_transposes(0, 1)
+        q_transposes(0)
+        q_transposes(1)
         k_regroup(0, 0, nc.vector.tensor_copy)
         k_regroup(0, 1, nc.scalar.copy)
+        q_regroup(0)
+        q_regroup(1)
+        k_quantise(0)
+        q_quantise(0)
+        q_quantise(1)
 
-        for step in range(-4, N_PAIRS + 7):
+        for step in range(-1, N_PAIRS + 7):
             run(scores, step + 1)
-            q_pairs = (step + 4,) if step not in (-2, -1) else (2, 3) if step == -1 else ()
+            q_pairs = (2, 3) if step == -1 else (step + 4,)
             for i in q_pairs:
                 run(q_transposes, i)
             if step in (3, 4):
@@ -310,34 +328,25 @@ def tile_multiheadattention_tupe_pb_t_kernel(tc, q, k, v, pos_bias, out_0, out_1
             run(add_pos, step)
             run(normalise, step - 2)
             run(row_maximum, step)
-            if step == 0:
-                v_regroup(0, 0)
-                v_regroup(0, 1)
             run(exp_bias, step)
-            if step == 0:
-                v_regroup(0, 2)
-                v_regroup(0, 3)
-                v_regroup(1, 0)
-                v_regroup(1, 1)
-            if step == 1:
-                v_regroup(1, 2)
-                v_regroup(1, 3)
             run(attn_transposes, step - 2)
             run(exponent, step - 1)
-            run(context_out, step - 6, step >= N_PAIRS)
+            if 1 <= step <= 4:
+                v_regroup((step - 1) // 2, 2 * ((step - 1) % 2))
+                v_regroup((step - 1) // 2, 2 * ((step - 1) % 2) + 1)
+            run(context_out, step - 5)
             for i in q_pairs:
                 run(q_regroup, i)
             if step in (3, 4):
                 k_regroup(1, step - 3, nc.scalar.copy)
             run(attn_regroup, step - 2)
-            if step == -2:
-                k_quantise(0)
             if step == 5:
                 k_quantise(1)
             if step == 3:
                 v_quantise(0)
-            if step == 4:
+            if step == 6:
                 v_quantise(1)
-            run(q_quantise, step + 3)
+            if step >= 0:
+                run(q_quantise, step + 3)
             run(attn_quantise, step - 3)
-            run(context_matmul, step - 5)
+            run(context_matmul, step - 4)

@@ -51,34 +51,31 @@ def tile_multiheadattention_tupe_pb_t_kernel(tc, q, k, v, pos_bias, out_0, out_1
                 part = slice(h * cols, (h + 1) * cols)
                 nc.sync.dma_start(out=table[key][:, part], in_=src[:, part])
 
-        def load_q(b, g):
-            load_queries(q_sb, (b, g), q[b, group_rows(g), :], "q_sb_%d_%d" % (b, g))
+        def load_q(b, g, parts=1):
+            load_queries(q_sb, (b, g), q[b, group_rows(g), :], "q_sb_%d_%d" % (b, g), parts)
 
         def load_pos(g):
             load_queries(pos_sb, g, pos_bias[group_rows(g), :], "pos_sb_%d" % g)
 
         def load_k(b):
             k_sb[b] = inputs.tile([P, SK // P, D], BF16, name="k_sb_%d" % b)
-            for h in range(2):
-                nc.sync.dma_start(
-                    out=k_sb[b][:, 2 * h : 2 * h + 2, :],
-                    in_=k[b, h * 2 * P : (h + 1) * 2 * P, :].rearrange("(j p) d -> p j d", p=P),
-                )
+            for j in range(SK // P):
+                nc.sync.dma_start(out=k_sb[b][:, j, :], in_=k[b, j * P : (j + 1) * P, :])
 
         def load_v(b):
             v_sb[b] = inputs.tile([P, PACK, D], BF16, name="v_sb_%d" % b)
             nc.sync.dma_start(out=v_sb[b][:], in_=v[b].rearrange("(t p) d -> p t d", p=P))
 
         load_k(0)
-        load_q(0, 0)
+        load_q(0, 0, parts=2)
         load_pos(0)
         load_q(0, 1)
         load_v(0)
-        load_v(1)
-        load_pos(1)
         load_q(0, 2)
-        load_pos(2)
+        load_pos(1)
+        load_v(1)
         load_q(0, 3)
+        load_pos(2)
         load_pos(3)
         load_k(1)
         for g in range(N_GROUPS):
@@ -127,7 +124,14 @@ def tile_multiheadattention_tupe_pb_t_kernel(tc, q, k, v, pos_bias, out_0, out_1
             if c == 0:
                 t["v_grouped", b] = keep.tile([P, D, PACK], BF16, name="v_grouped_%d" % b, align_bytes=64)
             cols = slice(c * P, (c + 1) * P)
-            nc.scalar.copy(out=t["v_grouped", b][:, cols, :], in_=v_sb[b][:].rearrange("p t d -> p d t")[:, cols, :])
+            source = v_sb[b][:].rearrange("p t d -> p d t")[:, cols, :]
+            if b == 0:
+                nc.gpsimd.tensor_scalar(
+                    out=t["v_grouped", b][:, cols, :], in0=source,
+                    scalar1=1.0, scalar2=0.0, op0=ALU.mult, op1=ALU.add,
+                )
+            else:
+                nc.scalar.copy(out=t["v_grouped", b][:, cols, :], in_=source)
 
         def v_quantise(b):
             codes = keep.tile([P, D], U32, name="v_codes_%d" % b, align_bytes=64)
@@ -237,11 +241,11 @@ def tile_multiheadattention_tupe_pb_t_kernel(tc, q, k, v, pos_bias, out_0, out_1
                     out=t["attn_sb", b, g][:, 2 * h + r, :], in0=t["e_sb", i][:, r, :],
                     scalar1=t["inv_sum", i][:, r : r + 1], scalar2=0.0, op0=ALU.mult, op1=ALU.add,
                 )
-            if h == 1:
-                nc.sync.dma_start(
-                    out=out_1[b, group_rows(g), :].rearrange("(p j) n -> p j n", j=GROUP),
-                    in_=t["attn_sb", b, g][:],
-                )
+            tiles = slice(2 * h, 2 * h + 2)
+            nc.sync.dma_start(
+                out=out_1[b, group_rows(g), :].rearrange("(p j) n -> p j n", j=GROUP)[:, tiles, :],
+                in_=t["attn_sb", b, g][:, tiles, :],
+            )
 
         def attn_transposes(i):
             b, g, h = place(i)
@@ -260,7 +264,7 @@ def tile_multiheadattention_tupe_pb_t_kernel(tc, q, k, v, pos_bias, out_0, out_1
                 t["a_grouped", b, g] = work.tile([P, 2 * PAIR_COLS], BF16, name="a_grouped", align_bytes=64)
             grouped = t["a_grouped", b, g][:].rearrange("p (j m x) -> p j m x", j=GROUP, x=PACK)
             for r in range(2):
-                copy = nc.vector.tensor_copy if i == N_PAIRS - 1 and r == 1 else nc.scalar.copy
+                copy = nc.vector.tensor_copy if r == 1 and i == N_PAIRS - 1 else nc.scalar.copy
                 copy(
                     out=grouped[:, 2 * h + r],
                     in_=t["attn_t", i, r][:].rearrange("p x m -> p m x"),
@@ -287,19 +291,19 @@ def tile_multiheadattention_tupe_pb_t_kernel(tc, q, k, v, pos_bias, out_0, out_1
                     stop=True,
                 )
 
-        def context_out(i):
+        def context_out(i, c):
             b, g, h = place(i)
-            if h == 0:
+            f = 2 * h + c
+            if f == 0:
                 t["ctx_sb", b, g] = results.tile([P, D // P, GROUP * P], F32, name="ctx_sb")
             ctx_sb = t["ctx_sb", b, g]
             rows = out_0[b].rearrange("(f p g) n -> g f p n", p=P, g=N_GROUPS)
-            for f in (2 * h, 2 * h + 1):
-                copy = nc.vector.tensor_copy if f % 2 == 1 else nc.scalar.copy
-                copy(
-                    out=ctx_sb[:, f, :].rearrange("p (m j) -> p m j", j=GROUP),
-                    in_=t["ctx_ps", b, g, f][:].rearrange("p (j m) -> p m j", j=GROUP),
-                )
-                nc.sync.dma_start(out=rows[g, f], in_=ctx_sb[:, f, :])
+            copy = nc.vector.tensor_copy if c == 1 and (f, g % 2) != (3, 1) else nc.scalar.copy
+            copy(
+                out=ctx_sb[:, f, :].rearrange("p (m j) -> p m j", j=GROUP),
+                in_=t["ctx_ps", b, g, f][:].rearrange("p (j m) -> p m j", j=GROUP),
+            )
+            nc.sync.dma_start(out=rows[g, f], in_=ctx_sb[:, f, :])
 
         def run(stage, i, *args):
             if 0 <= i < N_PAIRS:
@@ -317,13 +321,17 @@ def tile_multiheadattention_tupe_pb_t_kernel(tc, q, k, v, pos_bias, out_0, out_1
         q_quantise(0)
         q_quantise(1)
 
-        for step in range(-1, N_PAIRS + 7):
-            run(scores, step + 1)
+        for c in range(4):
+            v_regroup(0, c)
+        scores(0)
+        for step in range(-1, N_PAIRS):
             q_pairs = (2, 3) if step == -1 else (step + 4,)
             for i in q_pairs:
                 run(q_transposes, i)
-            if step in (3, 4):
-                k_transposes(1, step - 3)
+            if step in (4, 5):
+                k_transposes(1, step - 4)
+            if step >= 0:
+                run(scores, step + 1)
             run(reciprocal, step - 2)
             run(add_pos, step)
             run(normalise, step - 2)
@@ -331,22 +339,48 @@ def tile_multiheadattention_tupe_pb_t_kernel(tc, q, k, v, pos_bias, out_0, out_1
             run(exp_bias, step)
             run(attn_transposes, step - 2)
             run(exponent, step - 1)
-            if 1 <= step <= 4:
-                v_regroup((step - 1) // 2, 2 * ((step - 1) % 2))
-                v_regroup((step - 1) // 2, 2 * ((step - 1) % 2) + 1)
-            run(context_out, step - 5)
+            run(context_out, step - 5, 0)
+            run(context_out, step - 5, 1)
             for i in q_pairs:
                 run(q_regroup, i)
-            if step in (3, 4):
-                k_regroup(1, step - 3, nc.scalar.copy)
+            if step in (4, 5):
+                k_regroup(1, step - 4, nc.scalar.copy)
             run(attn_regroup, step - 2)
-            if step == 5:
-                k_quantise(1)
+            if 2 <= step <= 5:
+                v_regroup(1, step - 2)
             if step == 3:
                 v_quantise(0)
             if step == 6:
+                k_quantise(1)
+            if step == 8:
                 v_quantise(1)
             if step >= 0:
                 run(q_quantise, step + 3)
             run(attn_quantise, step - 3)
             run(context_matmul, step - 4)
+
+        n = N_PAIRS
+        exponent(n - 1)
+        reciprocal(n - 2)
+        normalise(n - 2)
+        context_out(n - 5, 0)
+        attn_transposes(n - 2)
+        attn_quantise(n - 3)
+        context_out(n - 5, 1)
+        attn_regroup(n - 2)
+        context_matmul(n - 4)
+        reciprocal(n - 1)
+        normalise(n - 1)
+        attn_transposes(n - 1)
+        context_out(n - 4, 0)
+        context_out(n - 4, 1)
+        context_matmul(n - 3)
+        attn_regroup(n - 1)
+        attn_quantise(n - 1)
+        context_out(n - 3, 0)
+        context_out(n - 3, 1)
+        context_matmul(n - 2)
+        context_matmul(n - 1)
+        for i in (n - 2, n - 1):
+            context_out(i, 0)
+            context_out(i, 1)

@@ -88,6 +88,14 @@ def tile_multiheadattention_tupe_pb_t_kernel(tc, q, k, v, pos_bias, out_0, out_1
         nc.vector.memset(zero[:], 0.0)
         nc.scalar.activation(out=one[:], in_=zero[:], func=EXP)
 
+        blank = const.tile([P, SK], BF16, name="blank")
+        nc.vector.memset(blank[:], 0.0)
+
+        def warm_up(count):
+            for c in range(count):
+                unused = psum.tile([P, SK], F32, name="ctx_ps")
+                nc.tensor.matmul(unused[:], blank[:, :P], blank[:], start=True, stop=True)
+
         def transpose_words(rows, r, words_t):
             words = rows.bitcast(F32)
             for u in range(2):
@@ -103,35 +111,42 @@ def tile_multiheadattention_tupe_pb_t_kernel(tc, q, k, v, pos_bias, out_0, out_1
             nc.vector.quantize_mx(out=codes.bitcast(FP8X4), scales=scales, in_=grouped)
 
         t = {}
+        on_vector, on_scalar = nc.vector.tensor_copy, nc.scalar.copy
 
-        def k_transposes(b, h):
-            t["k_words", b, h] = psum.tile([P, 2, 2, P], F32, name="words_t")
-            for r in range(2):
-                transpose_words(k_sb[b][:, 2 * h + r, :], r, t["k_words", b, h])
+        def k_transposes(b, j):
+            if j % 2 == 0:
+                t["k_words", b, j // 2] = psum.tile([P, 2, 2, P], F32, name="words_t")
+            transpose_words(k_sb[b][:, j, :], j % 2, t["k_words", b, j // 2])
 
-        def k_regroup(b, h, copy):
-            if h == 0:
+        def k_regroup(b, j, count, copy):
+            if j == 0:
                 t["k_grouped", b] = keep.tile([P, SK * PACK], BF16, name="k_grouped_%d" % b, align_bytes=64)
-            regroup_words(copy, t["k_words", b, h], t["k_grouped", b][:, h * PAIR_COLS : (h + 1) * PAIR_COLS])
+            blocks = slice(j % 2, j % 2 + count)
+            grouped = t["k_grouped", b][:].bitcast(F32).rearrange("p (j m u) -> p j m u", u=2, m=P)
+            copy(
+                out=grouped[:, j : j + count], in_=t["k_words", b, j // 2][:, blocks].rearrange("p r u m -> p r m u")
+            )
 
-        def k_quantise(b):
-            codes = keep.tile([P, SK], U32, name="k_codes_%d" % b, align_bytes=64)
-            scales = keep.tile([P, SK], U8, name="k_scales_%d" % b, align_bytes=64)
-            quantise(codes[:], scales[:], t["k_grouped", b][:])
-            t["k_mx", b] = codes, scales
+        def k_quantise(b, first, count):
+            if first == 0:
+                codes = keep.tile([P, SK], U32, name="k_codes_%d" % b, align_bytes=64)
+                scales = keep.tile([P, SK], U8, name="k_scales_%d" % b, align_bytes=64)
+                t["k_mx", b] = codes, scales
+            codes, scales = t["k_mx", b]
+            cols = slice(first * P, (first + count) * P)
+            quantise(codes[:, cols], scales[:, cols], t["k_grouped", b][:, first * P * PACK : (first + count) * P * PACK])
 
         def v_regroup(b, c):
             if c == 0:
                 t["v_grouped", b] = keep.tile([P, D, PACK], BF16, name="v_grouped_%d" % b, align_bytes=64)
             cols = slice(c * P, (c + 1) * P)
-            source = v_sb[b][:].rearrange("p t d -> p d t")[:, cols, :]
-            if b == 0:
-                nc.gpsimd.tensor_scalar(
-                    out=t["v_grouped", b][:, cols, :], in0=source,
-                    scalar1=1.0, scalar2=0.0, op0=ALU.mult, op1=ALU.add,
-                )
-            else:
-                nc.scalar.copy(out=t["v_grouped", b][:, cols, :], in_=source)
+            nc.scalar.copy(
+                out=t["v_grouped", b][:, cols, :], in_=v_sb[b][:].rearrange("p t d -> p d t")[:, cols, :]
+            )
+
+        def v_regroup_on_vector(b):
+            t["v_grouped", b] = keep.tile([P, D, PACK], BF16, name="v_grouped_%d" % b, align_bytes=64)
+            nc.vector.tensor_copy(out=t["v_grouped", b][:], in_=v_sb[b][:].rearrange("p t d -> p d t"))
 
         def v_quantise(b):
             codes = keep.tile([P, D], U32, name="v_codes_%d" % b, align_bytes=64)
@@ -149,32 +164,24 @@ def tile_multiheadattention_tupe_pb_t_kernel(tc, q, k, v, pos_bias, out_0, out_1
                 j = 2 * h + r
                 transpose_words(q_sb[b, g][:, j * D : (j + 1) * D], r, t["q_words", i])
 
-        def quantise_group(name, source, i):
-            b, g, h = place(i)
-            if h == 1:
-                codes = work.tile([P, GROUP * P], U32, name=name + "_codes", align_bytes=64)
-                scales = work.tile([P, GROUP * P], U8, name=name + "_scales", align_bytes=64)
-                quantise(codes[:], scales[:], t[source, b, g][:])
-                t[name, b, g] = codes, scales
+        def quantise_group(i, name, source):
+            quantise_tiles(name, source, i, 0, GROUP)
 
         def q_regroup(i):
             b, g, h = place(i)
             if h == 0:
                 t["q_grouped", b, g] = work.tile([P, 2 * PAIR_COLS], BF16, name="q_grouped", align_bytes=64)
             grouped = t["q_grouped", b, g][:, h * PAIR_COLS : (h + 1) * PAIR_COLS]
-            regroup_words(nc.vector.tensor_copy if i == 0 else nc.scalar.copy, t["q_words", i], grouped)
+            regroup_words(on_scalar, t["q_words", i], grouped)
 
-        def q_quantise(i):
-            if i >= 2:
-                quantise_group("q_mx", "q_grouped", i)
-                return
-            if i == 0:
-                codes = work.tile([P, GROUP * P], U32, name="q_mx_codes", align_bytes=64)
-                scales = work.tile([P, GROUP * P], U8, name="q_mx_scales", align_bytes=64)
-                t["q_mx", 0, 0] = codes, scales
-            codes, scales = t["q_mx", 0, 0]
-            cols = slice(i * 2 * P, (i + 1) * 2 * P)
-            quantise(codes[:, cols], scales[:, cols], t["q_grouped", 0, 0][:, i * PAIR_COLS : (i + 1) * PAIR_COLS])
+        def q_regroup_tile(r, copy):
+            if r == 0:
+                t["q_grouped", 0, 0] = work.tile([P, 2 * PAIR_COLS], BF16, name="q_grouped", align_bytes=64)
+            grouped = t["q_grouped", 0, 0][:, r * P * PACK : (r + 1) * P * PACK]
+            copy(
+                out=grouped.bitcast(F32).rearrange("p (m u) -> p m u", u=2),
+                in_=t["q_words", 0][:, r].rearrange("p u m -> p m u"),
+            )
 
         def scores(i):
             b, g, h = place(i)
@@ -217,61 +224,64 @@ def tile_multiheadattention_tupe_pb_t_kernel(tc, q, k, v, pos_bias, out_0, out_1
                 scalar1=-INV_SCALE, scalar2=0.0, op0=ALU.mult, op1=ALU.add,
             )
 
-        def exponent(i):
-            t["e_sb", i] = soft.tile([P, 2, SK], F32, name="e_sb")
-            t["row_sum", i] = soft.tile([P, 2], F32, name="row_sum")
-            for r in range(2):
-                nc.scalar.activation(
-                    out=t["e_sb", i][:, r, :], in_=t["s_sb", i][:, r, :], func=EXP,
-                    bias=t["exp_bias", i][:, r : r + 1], scale=INV_SCALE,
-                    accum_out=t["row_sum", i][:, r : r + 1],
-                )
+        def exponent(i, r):
+            if r == 0:
+                t["e_sb", i] = soft.tile([P, 2, SK], F32, name="e_sb")
+                t["row_sum", i] = soft.tile([P, 2], F32, name="row_sum")
+            nc.scalar.activation(
+                out=t["e_sb", i][:, r, :], in_=t["s_sb", i][:, r, :], func=EXP,
+                bias=t["exp_bias", i][:, r : r + 1], scale=INV_SCALE,
+                accum_out=t["row_sum", i][:, r : r + 1],
+            )
 
-        def reciprocal(i):
-            t["inv_sum", i] = soft.tile([P, 2], F32, name="inv_sum")
-            nc.vector.reciprocal(out=t["inv_sum", i][:], in_=t["row_sum", i][:])
+        def reciprocal(i, first, count):
+            if first == 0:
+                t["inv_sum", i] = soft.tile([P, 2], F32, name="inv_sum")
+            cols = slice(first, first + count)
+            nc.vector.reciprocal(out=t["inv_sum", i][:, cols], in_=t["row_sum", i][:, cols])
 
-        def normalise(i):
+        def normalise(i, r, multiply):
             b, g, h = place(i)
-            if h == 0:
+            if h == 0 and r == 0:
                 t["attn_sb", b, g] = results.tile([P, GROUP, SK], F32, name="attn_sb")
-            multiply = nc.gpsimd.tensor_scalar if i < N_PAIRS - 2 else nc.vector.tensor_scalar
-            for r in range(2):
-                multiply(
-                    out=t["attn_sb", b, g][:, 2 * h + r, :], in0=t["e_sb", i][:, r, :],
-                    scalar1=t["inv_sum", i][:, r : r + 1], scalar2=0.0, op0=ALU.mult, op1=ALU.add,
-                )
+            multiply(
+                out=t["attn_sb", b, g][:, 2 * h + r, :], in0=t["e_sb", i][:, r, :],
+                scalar1=t["inv_sum", i][:, r : r + 1], scalar2=0.0, op0=ALU.mult, op1=ALU.add,
+            )
+
+        def attn_store(i):
+            b, g, h = place(i)
             tiles = slice(2 * h, 2 * h + 2)
             nc.sync.dma_start(
                 out=out_1[b, group_rows(g), :].rearrange("(p j) n -> p j n", j=GROUP)[:, tiles, :],
                 in_=t["attn_sb", b, g][:, tiles, :],
             )
 
-        def attn_transposes(i):
+        def attn_transposes(i, r):
             b, g, h = place(i)
-            for r in range(2):
-                t["attn_t", i, r] = psum.tile([P, PACK, P], F32, name="attn_t")
-                for x in range(PACK):
-                    nc.tensor.transpose(
-                        t["attn_t", i, r][:, x, :],
-                        t["attn_sb", b, g][:, 2 * h + r, x * P : (x + 1) * P],
-                        ident[:],
-                    )
-
-        def attn_regroup(i):
-            b, g, h = place(i)
-            if h == 0:
-                t["a_grouped", b, g] = work.tile([P, 2 * PAIR_COLS], BF16, name="a_grouped", align_bytes=64)
-            grouped = t["a_grouped", b, g][:].rearrange("p (j m x) -> p j m x", j=GROUP, x=PACK)
-            for r in range(2):
-                copy = nc.vector.tensor_copy if r == 1 and i == N_PAIRS - 1 else nc.scalar.copy
-                copy(
-                    out=grouped[:, 2 * h + r],
-                    in_=t["attn_t", i, r][:].rearrange("p x m -> p m x"),
+            t["attn_t", i, r] = psum.tile([P, PACK, P], F32, name="attn_t")
+            for x in range(PACK):
+                nc.tensor.transpose(
+                    t["attn_t", i, r][:, x, :], t["attn_sb", b, g][:, 2 * h + r, x * P : (x + 1) * P], ident[:]
                 )
 
-        def attn_quantise(i):
-            quantise_group("a_mx", "a_grouped", i)
+        def attn_regroup(i, r, copy):
+            b, g, h = place(i)
+            if h == 0 and r == 0:
+                t["a_grouped", b, g] = work.tile([P, 2 * PAIR_COLS], BF16, name="a_grouped", align_bytes=64)
+            grouped = t["a_grouped", b, g][:].rearrange("p (j m x) -> p j m x", j=GROUP, x=PACK)
+            copy(out=grouped[:, 2 * h + r], in_=t["attn_t", i, r][:].rearrange("p x m -> p m x"))
+
+        def quantise_tiles(name, source, i, first, count):
+            b, g, h = place(i)
+            if first == 0:
+                codes = work.tile([P, GROUP * P], U32, name=name + "_codes", align_bytes=64)
+                scales = work.tile([P, GROUP * P], U8, name=name + "_scales", align_bytes=64)
+                t[name, b, g] = codes, scales
+            codes, scales = t[name, b, g]
+            cols = slice(first * P, (first + count) * P)
+            values = slice(first * P * PACK, (first + count) * P * PACK)
+            quantise(codes[:, cols], scales[:, cols], t[source, b, g][:, values])
 
         def context_matmul(i):
             b, g, h = place(i)
@@ -291,14 +301,13 @@ def tile_multiheadattention_tupe_pb_t_kernel(tc, q, k, v, pos_bias, out_0, out_1
                     stop=True,
                 )
 
-        def context_out(i, c):
+        def context_out(i, c, copy):
             b, g, h = place(i)
             f = 2 * h + c
             if f == 0:
                 t["ctx_sb", b, g] = results.tile([P, D // P, GROUP * P], F32, name="ctx_sb")
             ctx_sb = t["ctx_sb", b, g]
             rows = out_0[b].rearrange("(f p g) n -> g f p n", p=P, g=N_GROUPS)
-            copy = nc.vector.tensor_copy if c == 1 and (f, g % 2) != (3, 1) else nc.scalar.copy
             copy(
                 out=ctx_sb[:, f, :].rearrange("p (m j) -> p m j", j=GROUP),
                 in_=t["ctx_ps", b, g, f][:].rearrange("p (j m) -> p m j", j=GROUP),
@@ -309,78 +318,109 @@ def tile_multiheadattention_tupe_pb_t_kernel(tc, q, k, v, pos_bias, out_0, out_1
             if 0 <= i < N_PAIRS:
                 stage(i, *args)
 
-        k_transposes(0, 0)
-        k_transposes(0, 1)
+        def run_tiles(stage, i, *args):
+            for r in range(2):
+                run(stage, i, r, *args)
+
+        warm_up(6)
+        for j in range(SK // P):
+            k_transposes(0, j)
         q_transposes(0)
         q_transposes(1)
-        k_regroup(0, 0, nc.vector.tensor_copy)
-        k_regroup(0, 1, nc.scalar.copy)
-        q_regroup(0)
+        warm_up(2)
+        k_regroup(0, 0, 1, on_vector)
+        k_regroup(0, 1, 1, on_scalar)
+        k_regroup(0, 2, 1, on_vector)
+        k_regroup(0, 3, 1, on_scalar)
+        k_quantise(0, 0, 2)
+        q_regroup_tile(0, on_vector)
+        q_regroup_tile(1, on_scalar)
+        k_quantise(0, 2, 2)
+        quantise_tiles("q_mx", "q_grouped", 0, 0, 2)
         q_regroup(1)
-        k_quantise(0)
-        q_quantise(0)
-        q_quantise(1)
+        quantise_tiles("q_mx", "q_grouped", 0, 2, 2)
 
-        for c in range(4):
-            v_regroup(0, c)
         scores(0)
         for step in range(-1, N_PAIRS):
-            q_pairs = (2, 3) if step == -1 else (step + 4,)
+            last = step == N_PAIRS - 1
+            q_pairs = {-1: (2, 3), 0: (), 1: (4, 5)}.get(step, (step + 4,))
             for i in q_pairs:
                 run(q_transposes, i)
             if step in (4, 5):
-                k_transposes(1, step - 4)
+                k_transposes(1, 2 * (step - 4))
+                k_transposes(1, 2 * (step - 4) + 1)
             if step >= 0:
                 run(scores, step + 1)
-            run(reciprocal, step - 2)
+            run(reciprocal, step - 2, 0, 2)
             run(add_pos, step)
-            run(normalise, step - 2)
+            run_tiles(normalise, step - 2, nc.gpsimd.tensor_scalar)
+            run(attn_store, step - 2)
             run(row_maximum, step)
             run(exp_bias, step)
-            run(attn_transposes, step - 2)
-            run(exponent, step - 1)
-            run(context_out, step - 5, 0)
-            run(context_out, step - 5, 1)
+            if step == 5:
+                v_regroup_on_vector(1)
+            run_tiles(attn_transposes, step - 2)
+            run_tiles(exponent, step - 1)
+            run(context_out, step - 5, 0, on_scalar)
+            if not last:
+                run(context_out, step - 5, 1, on_vector if step % 2 == 0 else on_scalar)
             for i in q_pairs:
                 run(q_regroup, i)
+            for c in {0: (0, 1), 1: (2,), 2: (3,)}.get(step, ()):
+                v_regroup(0, c)
             if step in (4, 5):
-                k_regroup(1, step - 4, nc.scalar.copy)
-            run(attn_regroup, step - 2)
-            if 2 <= step <= 5:
-                v_regroup(1, step - 2)
+                k_regroup(1, 2 * (step - 4), 2, on_scalar)
+            if not last:
+                run_tiles(attn_regroup, step - 2, on_scalar)
             if step == 3:
                 v_quantise(0)
             if step == 6:
-                k_quantise(1)
-            if step == 8:
+                k_quantise(1, 0, 4)
+            if step == 10:
                 v_quantise(1)
-            if step >= 0:
-                run(q_quantise, step + 3)
-            run(attn_quantise, step - 3)
+            if step % 2 == 0:
+                run(quantise_group, step + 2, "q_mx", "q_grouped")
+                run(quantise_group, step - 4, "a_mx", "a_grouped")
             run(context_matmul, step - 4)
 
         n = N_PAIRS
-        exponent(n - 1)
-        reciprocal(n - 2)
-        normalise(n - 2)
-        context_out(n - 5, 0)
-        attn_transposes(n - 2)
-        attn_quantise(n - 3)
-        context_out(n - 5, 1)
-        attn_regroup(n - 2)
+        x, y, z = n - 3, n - 2, n - 1
+        on_v = nc.vector.tensor_scalar
+        context_out(n - 6, 1, on_vector)
+        attn_regroup(x, 0, on_scalar)
+        attn_regroup(x, 1, on_vector)
+        exponent(z, 0)
+        reciprocal(y, 0, 2)
+        normalise(y, 0, on_v)
+        normalise(y, 1, on_v)
+        attn_store(y)
+        exponent(z, 1)
+        attn_transposes(y, 0)
+        attn_transposes(y, 1)
+        quantise_tiles("a_mx", "a_grouped", x, 0, GROUP)
+        reciprocal(z, 0, 1)
+        context_out(n - 5, 0, on_scalar)
         context_matmul(n - 4)
-        reciprocal(n - 1)
-        normalise(n - 1)
-        attn_transposes(n - 1)
-        context_out(n - 4, 0)
-        context_out(n - 4, 1)
+        normalise(z, 0, on_v)
+        attn_regroup(y, 0, on_scalar)
+        attn_regroup(y, 1, on_scalar)
+        reciprocal(z, 1, 1)
+        context_out(n - 5, 1, on_vector)
+        normalise(z, 1, on_v)
+        attn_store(z)
+        attn_transposes(z, 0)
+        attn_transposes(z, 1)
+        context_out(n - 4, 0, on_scalar)
+        context_out(n - 4, 1, on_vector)
         context_matmul(n - 3)
-        attn_regroup(n - 1)
-        attn_quantise(n - 1)
-        context_out(n - 3, 0)
-        context_out(n - 3, 1)
+        attn_regroup(z, 0, on_scalar)
+        quantise_tiles("a_mx", "a_grouped", y, 0, 2)
+        attn_regroup(z, 1, on_vector)
+        context_out(n - 3, 0, on_scalar)
+        context_out(n - 3, 1, on_vector)
+        quantise_tiles("a_mx", "a_grouped", z, 2, 2)
         context_matmul(n - 2)
         context_matmul(n - 1)
         for i in (n - 2, n - 1):
-            context_out(i, 0)
-            context_out(i, 1)
+            context_out(i, 0, on_scalar)
+            context_out(i, 1, on_vector)

@@ -206,8 +206,8 @@ def tile_multiheadattention_tupe_pb_t_kernel(tc, q, k, v, pos_bias, out_0, out_1
             for r in range(2):
                 j = 2 * h + r
                 nc.vector.tensor_tensor(
-                    out=t["s_sb", i][:, r, :], in0=t["score_ps", i, r][:],
-                    in1=pos_sb[g][:, j * SK : (j + 1) * SK], op=ALU.add,
+                    out=t["s_sb", i][:, r, :], in0=pos_sb[g][:, j * SK : (j + 1) * SK],
+                    in1=t["score_ps", i, r][:], op=ALU.add,
                 )
 
         def row_maximum(i):

@@ -93,7 +93,7 @@ def tile_multiheadattention_tupe_pb_t_kernel(tc, q, k, v, pos_bias, out_0, out_1
 
         def warm_up(count):
             for c in range(count):
-                unused = psum.tile([P, SK], F32, name="ctx_ps")
+                unused = psum.tile([P, SK], F32, name="words_t")
                 nc.tensor.matmul(unused[:], blank[:, :P], blank[:], start=True, stop=True)
 
         def transpose_words(rows, r, words_t):
@@ -360,6 +360,8 @@ def tile_multiheadattention_tupe_pb_t_kernel(tc, q, k, v, pos_bias, out_0, out_1
             if step == 5:
                 v_regroup_on_vector(1)
             run_tiles(attn_transposes, step - 2)
+            if step >= 2:
+                warm_up(1)
             run_tiles(exponent, step - 1)
             run(context_out, step - 5, 0, on_scalar)
             if not last:

import math
from contextlib import ExitStack

import concourse.masks as masks
import concourse.mybir as mybir

F32 = mybir.dt.float32
BF16 = mybir.dt.bfloat16
U32 = mybir.dt.uint32
U8 = mybir.dt.uint8
FP8X4 = mybir.dt.float8_e4m3fn_x4
ALU = mybir.AluOpType
EXP = mybir.ActivationFunctionType.Exp
AXIS_X = mybir.AxisListType.X

B, SQ, SK, D = 2, 2048, 512, 512
P = 128
PACK = 4
GROUP = 4
N_GROUPS = SQ // (GROUP * P)
PAIR_COLS = 2 * P * PACK
N_PAIRS = B * SQ // (2 * P)
PAIRS_PER_BATCH = N_PAIRS // B
INV_SCALE = 1.0 / math.sqrt(2.0 * 64.0)

FLOPS = 2 * (2 * B * SQ * SK * D)


def tile_multiheadattention_tupe_pb_t_kernel(tc, q, k, v, pos_bias, out_0, out_1):
    nc = tc.nc
    with ExitStack() as ctx:
        const = ctx.enter_context(tc.tile_pool(name="const", bufs=1))
        inputs = ctx.enter_context(tc.tile_pool(name="inputs", bufs=1))
        keep = ctx.enter_context(tc.tile_pool(name="keep", bufs=1))
        work = ctx.enter_context(tc.tile_pool(name="work", bufs=4))
        soft = ctx.enter_context(tc.tile_pool(name="soft", bufs=4))
        results = ctx.enter_context(tc.tile_pool(name="results", bufs=3))
        psum = ctx.enter_context(tc.psum_pool(name="psum", bufs=2))
        ctx.enter_context(tc.manual_schedule())

        def group_rows(g):
            return slice(g * GROUP * P, (g + 1) * GROUP * P)

        q_sb, pos_sb, k_sb, v_sb = {}, {}, {}, {}

        def load_queries(table, key, rows, name, parts=1):
            table[key] = inputs.tile([P, GROUP * 512], BF16, name=name)
            cols = GROUP * 512 // parts
            src = rows.rearrange("(p j) d -> p (j d)", j=GROUP)
            for h in range(parts):
                part = slice(h * cols, (h + 1) * cols)
                nc.sync.dma_start(out=table[key][:, part], in_=src[:, part])

        def load_q(b, g, parts=1):
            load_queries(q_sb, (b, g), q[b, group_rows(g), :], "q_sb_%d_%d" % (b, g), parts)

        def load_pos(g):
            load_queries(pos_sb, g, pos_bias[group_rows(g), :], "pos_sb_%d" % g)

        def load_k(b):
            k_sb[b] = inputs.tile([P, SK // P, D], BF16, name="k_sb_%d" % b)
            for j in range(SK // P):
                nc.sync.dma_start(out=k_sb[b][:, j, :], in_=k[b, j * P : (j + 1) * P, :])

        def load_v(b):
            v_sb[b] = inputs.tile([P, PACK, D], BF16, name="v_sb_%d" % b)
            nc.sync.dma_start(out=v_sb[b][:], in_=v[b].rearrange("(t p) d -> p t d", p=P))

        load_k(0)
        load_q(0, 0, parts=2)
        load_pos(0)
        load_q(0, 1)
        load_v(0)
        load_q(0, 2)
        load_pos(1)
        load_v(1)
        load_q(0, 3)
        load_pos(2)
        load_pos(3)
        load_k(1)
        for g in range(N_GROUPS):
            load_q(1, g)

        ident = const.tile([P, P], F32, name="ident")
        masks.make_identity(nc, ident[:])
        zero = const.tile([P, 1], F32, name="zero")
        one = const.tile([P, 1], F32, name="one")
        nc.vector.memset(zero[:], 0.0)
        nc.scalar.activation(out=one[:], in_=zero[:], func=EXP)

        blank = const.tile([P, SK], BF16, name="blank")
        nc.vector.memset(blank[:], 0.0)

        def warm_up(count):
            for c in range(count):
                unused = psum.tile([P, SK], F32, name="words_t")
                nc.tensor.matmul(unused[:], blank[:, :P], blank[:], start=True, stop=True)

        def transpose_words(rows, r, words_t):
            words = rows.bitcast(F32)
            for u in range(2):
                nc.tensor.transpose(words_t[:, r, u, :], words[:, u * P : (u + 1) * P], ident[:])

        def regroup_words(copy, words_t, grouped):
            copy(
                out=grouped.bitcast(F32).rearrange("p (r m u) -> p r m u", r=2, u=2),
                in_=words_t[:].rearrange("p r u m -> p r m u"),
            )

        def quantise(codes, scales, grouped):
            nc.vector.quantize_mx(out=codes.bitcast(FP8X4), scales=scales, in_=grouped)

        t = {}
        on_vector, on_scalar = nc.vector.tensor_copy, nc.scalar.copy

        def k_transposes(b, j):
            if j % 2 == 0:
                t["k_words", b, j // 2] = psum.tile([P, 2, 2, P], F32, name="words_t")
            transpose_words(k_sb[b][:, j, :], j % 2, t["k_words", b, j // 2])

        def k_regroup(b, j, count, copy):
            if j == 0:
                t["k_grouped", b] = keep.tile([P, SK * PACK], BF16, name="k_grouped_%d" % b, align_bytes=64)
            blocks = slice(j % 2, j % 2 + count)
            grouped = t["k_grouped", b][:].bitcast(F32).rearrange("p (j m u) -> p j m u", u=2, m=P)
            copy(
                out=grouped[:, j : j + count], in_=t["k_words", b, j // 2][:, blocks].rearrange("p r u m -> p r m u")
            )

        def k_quantise(b, first, count):
            if first == 0:
                codes = keep.tile([P, SK], U32, name="k_codes_%d" % b, align_bytes=64)
                scales = keep.tile([P, SK], U8, name="k_scales_%d" % b, align_bytes=64)
                t["k_mx", b] = codes, scales
            codes, scales = t["k_mx", b]
            cols = slice(first * P, (first + count) * P)
            quantise(codes[:, cols], scales[:, cols], t["k_grouped", b][:, first * P * PACK : (first + count) * P * PACK])

        def v_regroup(b, c):
            if c == 0:
                t["v_grouped", b] = keep.tile([P, D, PACK], BF16, name="v_grouped_%d" % b, align_bytes=64)
            cols = slice(c * P, (c + 1) * P)
            nc.scalar.copy(
                out=t["v_grouped", b][:, cols, :], in_=v_sb[b][:].rearrange("p t d -> p d t")[:, cols, :]
            )

        def v_regroup_on_vector(b):
            t["v_grouped", b] = keep.tile([P, D, PACK], BF16, name="v_grouped_%d" % b, align_bytes=64)
            nc.vector.tensor_copy(out=t["v_grouped", b][:], in_=v_sb[b][:].rearrange("p t d -> p d t"))

        def v_quantise(b):
            codes = keep.tile([P, D], U32, name="v_codes_%d" % b, align_bytes=64)
            scales = keep.tile([P, D], U8, name="v_scales_%d" % b, align_bytes=64)
            quantise(codes[:], scales[:], t["v_grouped", b][:].rearrange("p d t -> p (d t)"))
            t["v_mx", b] = codes, scales

        def place(i):
            return i // PAIRS_PER_BATCH, (i % PAIRS_PER_BATCH) // 2, i % 2

        def q_transposes(i):
            b, g, h = place(i)
            t["q_words", i] = psum.tile([P, 2, 2, P], F32, name="attn_t" if i < 2 else "words_t")
            for r in range(2):
                j = 2 * h + r
                transpose_words(q_sb[b, g][:, j * D : (j + 1) * D], r, t["q_words", i])

        def quantise_group(i, name, source):
            quantise_tiles(name, source, i, 0, GROUP)

        def q_regroup(i):
            b, g, h = place(i)
            if h == 0:
                t["q_grouped", b, g] = work.tile([P, 2 * PAIR_COLS], BF16, name="q_grouped", align_bytes=64)
            grouped = t["q_grouped", b, g][:, h * PAIR_COLS : (h + 1) * PAIR_COLS]
            regroup_words(on_scalar, t["q_words", i], grouped)

        def q_regroup_tile(r, copy):
            if r == 0:
                t["q_grouped", 0, 0] = work.tile([P, 2 * PAIR_COLS], BF16, name="q_grouped", align_bytes=64)
            grouped = t["q_grouped", 0, 0][:, r * P * PACK : (r + 1) * P * PACK]
            copy(
                out=grouped.bitcast(F32).rearrange("p (m u) -> p m u", u=2),
                in_=t["q_words", 0][:, r].rearrange("p u m -> p m u"),
            )

        def scores(i):
            b, g, h = place(i)
            q_codes, q_scales = t["q_mx", b, g]
            k_codes, k_scales = t["k_mx", b]
            for r in range(2):
                cols = slice((2 * h + r) * P, (2 * h + r + 1) * P)
                t["score_ps", i, r] = psum.tile([P, SK], F32, name="score_ps")
                nc.tensor.matmul_mx(
                    out=t["score_ps", i, r][:],
                    lhsT=q_codes[:, cols].bitcast(FP8X4),
                    lhsT_scale=q_scales[:, cols],
                    rhs=k_codes[:].bitcast(FP8X4),
                    rhs_scale=k_scales[:],
                    start=True,
                    stop=True,
                )

        def add_pos(i):
            g, h = place(i)[1:]
            t["s_sb", i] = soft.tile([P, 2, SK], F32, name="s_sb")
            for r in range(2):
                j = 2 * h + r
                nc.vector.tensor_tensor(
                    out=t["s_sb", i][:, r, :], in0=pos_sb[g][:, j * SK : (j + 1) * SK],
                    in1=t["score_ps", i, r][:], op=ALU.add,
                )

        def row_maximum(i):
            t["row_max", i] = soft.tile([P, 2], F32, name="row_max")
            for r in range(2):
                nc.vector.tensor_reduce(
                    out=t["row_max", i][:, r : r + 1], in_=t["s_sb", i][:, r, :], axis=AXIS_X, op=ALU.max
                )

        def exp_bias(i):
            t["exp_bias", i] = soft.tile([P, 2], F32, name="exp_bias")
            nc.gpsimd.tensor_scalar(
                out=t["exp_bias", i][:], in0=t["row_max", i][:],
                scalar1=-INV_SCALE, scalar2=0.0, op0=ALU.mult, op1=ALU.add,
            )

        def exponent(i, r):
            if r == 0:
                t["e_sb", i] = soft.tile([P, 2, SK], F32, name="e_sb")
                t["row_sum", i] = soft.tile([P, 2], F32, name="row_sum")
            nc.scalar.activation(
                out=t["e_sb", i][:, r, :], in_=t["s_sb", i][:, r, :], func=EXP,
                bias=t["exp_bias", i][:, r : r + 1], scale=INV_SCALE,
                accum_out=t["row_sum", i][:, r : r + 1],
            )

        def reciprocal(i, first, count):
            if first == 0:
                t["inv_sum", i] = soft.tile([P, 2], F32, name="inv_sum")
            cols = slice(first, first + count)
            nc.vector.reciprocal(out=t["inv_sum", i][:, cols], in_=t["row_sum", i][:, cols])

        def normalise(i, r, multiply):
            b, g, h = place(i)
            if h == 0 and r == 0:
                t["attn_sb", b, g] = results.tile([P, GROUP, SK], F32, name="attn_sb")
            multiply(
                out=t["attn_sb", b, g][:, 2 * h + r, :], in0=t["e_sb", i][:, r, :],
                scalar1=t["inv_sum", i][:, r : r + 1], scalar2=0.0, op0=ALU.mult, op1=ALU.add,
            )

        def attn_store(i):
            b, g, h = place(i)
            tiles = slice(2 * h, 2 * h + 2)
            nc.sync.dma_start(
                out=out_1[b, group_rows(g), :].rearrange("(p j) n -> p j n", j=GROUP)[:, tiles, :],
                in_=t["attn_sb", b, g][:, tiles, :],
            )

        def attn_transposes(i, r):
            b, g, h = place(i)
            t["attn_t", i, r] = psum.tile([P, PACK, P], F32, name="attn_t")
            for x in range(PACK):
                nc.tensor.transpose(
                    t["attn_t", i, r][:, x, :], t["attn_sb", b, g][:, 2 * h + r, x * P : (x + 1) * P], ident[:]
                )

        def attn_regroup(i, r, copy):
            b, g, h = place(i)
            if h == 0 and r == 0:
                t["a_grouped", b, g] = work.tile([P, 2 * PAIR_COLS], BF16, name="a_grouped", align_bytes=64)
            grouped = t["a_grouped", b, g][:].rearrange("p (j m x) -> p j m x", j=GROUP, x=PACK)
            copy(out=grouped[:, 2 * h + r], in_=t["attn_t", i, r][:].rearrange("p x m -> p m x"))

        def quantise_tiles(name, source, i, first, count):
            b, g, h = place(i)
            if first == 0:
                codes = work.tile([P, GROUP * P], U32, name=name + "_codes", align_bytes=64)
                scales = work.tile([P, GROUP * P], U8, name=name + "_scales", align_bytes=64)
                t[name, b, g] = codes, scales
            codes, scales = t[name, b, g]
            cols = slice(first * P, (first + count) * P)
            values = slice(first * P * PACK, (first + count) * P * PACK)
            quantise(codes[:, cols], scales[:, cols], t[source, b, g][:, values])

        def context_matmul(i):
            b, g, h = place(i)
            a_codes, a_scales = t["a_mx", b, g]
            v_codes, v_scales = t["v_mx", b]
            for f in (2 * h, 2 * h + 1):
                cols = slice(f * P, (f + 1) * P)
                name = "score_ps" if i >= N_PAIRS - 4 and f % 2 == 1 else "ctx_ps"
                t["ctx_ps", b, g, f] = psum.tile([P, GROUP * P], F32, name=name)
                nc.tensor.matmul_mx(
                    out=t["ctx_ps", b, g, f][:],
                    lhsT=v_codes[:, cols].bitcast(FP8X4),
                    lhsT_scale=v_scales[:, cols],
                    rhs=a_codes[:].bitcast(FP8X4),
                    rhs_scale=a_scales[:],
                    start=True,
                    stop=True,
                )

        def context_out(i, c, copy):
            b, g, h = place(i)
            f = 2 * h + c
            if f == 0:
                t["ctx_sb", b, g] = results.tile([P, D // P, GROUP * P], F32, name="ctx_sb")
            ctx_sb = t["ctx_sb", b, g]
            rows = out_0[b].rearrange("(f p g) n -> g f p n", p=P, g=N_GROUPS)
            copy(
                out=ctx_sb[:, f, :].rearrange("p (m j) -> p m j", j=GROUP),
                in_=t["ctx_ps", b, g, f][:].rearrange("p (j m) -> p m j", j=GROUP),
            )
            nc.sync.dma_start(out=rows[g, f], in_=ctx_sb[:, f, :])

        def run(stage, i, *args):
            if 0 <= i < N_PAIRS:
                stage(i, *args)

        def run_tiles(stage, i, *args):
            for r in range(2):
                run(stage, i, r, *args)

        warm_up(6)
        for j in range(SK // P):
            k_transposes(0, j)
        q_transposes(0)
        q_transposes(1)
        warm_up(2)
        k_regroup(0, 0, 1, on_vector)
        k_regroup(0, 1, 1, on_scalar)
        k_regroup(0, 2, 1, on_vector)
        k_regroup(0, 3, 1, on_scalar)
        k_quantise(0, 0, 2)
        q_regroup_tile(0, on_vector)
        q_regroup_tile(1, on_scalar)
        k_quantise(0, 2, 2)
        quantise_tiles("q_mx", "q_grouped", 0, 0, 2)
        q_regroup(1)
        quantise_tiles("q_mx", "q_grouped", 0, 2, 2)

        scores(0)
        for step in range(-1, N_PAIRS):
            last = step == N_PAIRS - 1
            q_pairs = {-1: (2, 3), 0: (), 1: (4, 5)}.get(step, (step + 4,))
            for i in q_pairs:
                run(q_transposes, i)
            if step in (4, 5):
                k_transposes(1, 2 * (step - 4))
                k_transposes(1, 2 * (step - 4) + 1)
            if step >= 0:
                run(scores, step + 1)
            run(reciprocal, step - 2, 0, 2)
            run(add_pos, step)
            run_tiles(normalise, step - 2, nc.gpsimd.tensor_scalar)
            run(attn_store, step - 2)
            run(row_maximum, step)
            run(exp_bias, step)
            if step == 5:
                v_regroup_on_vector(1)
            run_tiles(attn_transposes, step - 2)
            if step >= 2:
                warm_up(1)
            run_tiles(exponent, step - 1)
            run(context_out, step - 5, 0, on_scalar)
            if not last:
                run(context_out, step - 5, 1, on_vector if step % 2 == 0 else on_scalar)
            for i in q_pairs:
                run(q_regroup, i)
            for c in {0: (0, 1), 1: (2,), 2: (3,)}.get(step, ()):
                v_regroup(0, c)
            if step in (4, 5):
                k_regroup(1, 2 * (step - 4), 2, on_scalar)
            if not last:
                run_tiles(attn_regroup, step - 2, on_scalar)
            if step == 3:
                v_quantise(0)
            if step == 6:
                k_quantise(1, 0, 4)
            if step == 10:
                v_quantise(1)
            if step % 2 == 0:
                run(quantise_group, step + 2, "q_mx", "q_grouped")
                run(quantise_group, step - 4, "a_mx", "a_grouped")
            run(context_matmul, step - 4)

        n = N_PAIRS
        x, y, z = n - 3, n - 2, n - 1
        on_v = nc.vector.tensor_scalar
        context_out(n - 6, 1, on_vector)
        attn_regroup(x, 0, on_scalar)
        attn_regroup(x, 1, on_vector)
        exponent(z, 0)
        reciprocal(y, 0, 2)
        normalise(y, 0, on_v)
        normalise(y, 1, on_v)
        attn_store(y)
        exponent(z, 1)
        attn_transposes(y, 0)
        attn_transposes(y, 1)
        quantise_tiles("a_mx", "a_grouped", x, 0, GROUP)
        reciprocal(z, 0, 1)
        context_out(n - 5, 0, on_scalar)
        context_matmul(n - 4)
        normalise(z, 0, on_v)
        attn_regroup(y, 0, on_scalar)
        attn_regroup(y, 1, on_scalar)
        reciprocal(z, 1, 1)
        context_out(n - 5, 1, on_vector)
        normalise(z, 1, on_v)
        attn_store(z)
        attn_transposes(z, 0)
        attn_transposes(z, 1)
        context_out(n - 4, 0, on_scalar)
        context_out(n - 4, 1, on_vector)
        context_matmul(n - 3)
        attn_regroup(z, 0, on_scalar)
        quantise_tiles("a_mx", "a_grouped", y, 0, 2)
        attn_regroup(z, 1, on_vector)
        context_out(n - 3, 0, on_scalar)
        context_out(n - 3, 1, on_vector)
        quantise_tiles("a_mx", "a_grouped", z, 2, 2)
        context_matmul(n - 2)
        context_matmul(n - 1)
        for i in (n - 2, n - 1):
            context_out(i, 0, on_scalar)
            context_out(i, 1, on_vector)
